import numpy as np
import ml_dtypes


def mxq(x, axis, fmt="e4m3"):
    dtype, down = {"e4m3": (ml_dtypes.float8_e4m3fn, 7), "e5m2": (ml_dtypes.float8_e5m2, 14)}[fmt]
    v = np.moveaxis(np.asarray(x, np.float32).astype(ml_dtypes.bfloat16).astype(np.float64), axis, -1)
    blocks = v.reshape(v.shape[:-1] + (-1, 32))
    amax = np.abs(blocks).max(-1, keepdims=True)
    byte = np.maximum(np.where(amax > 0, np.frexp(amax)[1] - 1 + 127, 0) - down, 1)
    scale = np.exp2(byte - 127.0)
    codes = (blocks / scale).astype(np.float32).astype(dtype).astype(np.float64)
    return np.moveaxis((codes * scale).reshape(v.shape), -1, axis)


WIDE = False


def mx_kscale(k):
    if not WIDE:
        return np.ones(k)
    levels = np.array([10, -10, 5, -5, 0])
    a = np.random.permutation(np.resize(levels, k // 512 * 4)).reshape(k // 512, 4)
    idx = np.arange(k)
    return np.exp2(a[idx // 512, idx % 128 // 32])


BF16 = ml_dtypes.bfloat16


def bf(x):
    return np.asarray(x, np.float32).astype(BF16)


def f64(x):
    return np.asarray(x).astype(np.float64)


B, N, AB, MAXN, BB, H = 2, 32, 352, 255, 32, 1024
TAIL = AB - (MAXN + 1)
AF = AB + TAIL
FB = AF + BB + BB


def setup_inputs():
    s = mx_kscale(FB)
    sa, sb = s[:AB], s[AF:AF + BB]
    se = np.concatenate([sa, sa[MAXN + 1:], sb, sb])
    return {"f_atoms": bf(np.random.standard_normal((B, N, AB)) * sa),
            "f_bonds": bf(np.random.standard_normal((B, N, N, BB)) * sb),
            "adj": bf(np.random.uniform(size=(B, N, N)) * 4.0 / N),
            "W_i_w": bf(np.random.standard_normal((H, FB)) * 0.1 * N / np.sqrt(FB) / se)}


def reference(f_atoms, f_bonds, adj, W_i_w):
    f_atoms, f_bonds, adj = f64(f_atoms), f64(f_bonds), f64(adj)
    fa = np.concatenate([f_atoms, f_atoms[:, :, MAXN + 1:]], axis=-1)
    fa_exp = np.broadcast_to(fa[:, :, None, :], (B, N, N, AF))
    fb = np.concatenate([fa_exp, f_bonds, f_bonds], axis=-1)
    return mxq(adj[..., None] * fb, 3, "e4m3") @ mxq(f64(W_i_w).T, 0, "e4m3")

@@ -1,0 +1,202 @@
+from contextlib import ExitStack
+
+import concourse.mybir as mybir
+from concourse.masks import make_identity
+
+F32 = mybir.dt.float32
+BF16 = mybir.dt.bfloat16
+U32 = mybir.dt.uint32
+U8 = mybir.dt.uint8
+FP8X4 = mybir.dt.float8_e4m3fn_x4
+
+P = 128
+PACK = 4
+TILES = 16
+ATOM_F = 352
+TAIL_START = 256
+ATOM_COLS = ATOM_F + (ATOM_F - TAIL_START)
+BOND_F = 32
+F = ATOM_COLS + 2 * BOND_F
+H = 1024
+ATOM_K = ATOM_COLS // PACK
+BOND_K = BOND_F // PACK
+N_PASS = 512
+W_GROUPS = 4
+W_GROUP_H = H // W_GROUPS
+ROUND = 4
+BANK_TILES = 2
+STEPS = TILES // BANK_TILES
+AHEAD = 2
+
+FLOPS = 2 * P * TILES * F * H
+
+
+def tile_mpnencoder_pa_kernel(tc, f_atoms, f_bonds, adj, W_i_w, out):
+    nc = tc.nc
+
+    atom_rows = f_atoms.rearrange("b m f -> (b m) f")
+    bond_rows = f_bonds.rearrange("b m (s t) c -> (b m s) (t c)", s=2)
+    adj_rows = adj.rearrange("b m (s t) -> (b m s) t", s=2)
+    out_rows = out.rearrange("b m (s t) h -> (b m s) t h", s=2)
+    w_rows = W_i_w.rearrange("(g p r) f -> g p (r f)", p=P, r=2)
+
+    with ExitStack() as ctx:
+        keep = ctx.enter_context(tc.tile_pool(name="keep", bufs=1))
+        results = ctx.enter_context(tc.tile_pool(name="results", bufs=4))
+        adj_psum = ctx.enter_context(tc.psum_pool(name="adj_psum", bufs=1))
+        turn_psum = ctx.enter_context(tc.psum_pool(name="turn_psum", bufs=2))
+        acc_psum = ctx.enter_context(tc.psum_pool(name="acc_psum", bufs=5))
+        ctx.enter_context(tc.manual_schedule())
+
+        adj_cols = keep.tile([P, TILES], BF16)
+        nc.scalar.dma_start(out=adj_cols[:], in_=adj_rows)
+        atoms = keep.tile([P, ATOM_COLS], BF16)
+        for s in range(2):
+            nc.scalar.dma_start(out=atoms[s:P:2, 0:ATOM_F], in_=atom_rows)
+            nc.scalar.dma_start(
+                out=atoms[s:P:2, ATOM_F:ATOM_COLS], in_=atom_rows[:, TAIL_START:ATOM_F]
+            )
+        bonds = keep.tile([P, TILES * BOND_F], BF16)
+        nc.scalar.dma_start(out=bonds[:], in_=bond_rows)
+        w_sb = keep.tile([P, W_GROUPS, 2, F], BF16)
+        for g in range(W_GROUPS):
+            nc.sync.dma_start(out=w_sb[:, g].rearrange("p r f -> p (r f)"), in_=w_rows[g])
+
+        identity = keep.tile([P, P], F32)
+        make_identity(nc, identity[:])
+
+        features = keep.tile([P, TILES, 2, P], F32)
+        adj_twice = keep.tile([P, TILES, 2], BF16)
+        adj_spread = keep.tile([P, TILES, P], F32)
+        g_grouped = keep.tile([P, TILES, P * PACK], BF16, align_bytes=64)
+        g_codes = keep.tile([P, TILES * P], U32, align_bytes=64)
+        g_scales = keep.tile([P, TILES * P], U8, align_bytes=64)
+        w_grouped = keep.tile([P, H * PACK], BF16, align_bytes=64)
+        w_codes = keep.tile([P, H], U32, align_bytes=64)
+        w_scales = keep.tile([P, H], U8, align_bytes=64)
+
+        atom_words = atoms[:].bitcast(F32).rearrange("p (k u) -> p u k", u=2)
+        bond_words = bonds[:].bitcast(F32).rearrange("p (t k u) -> p t u k", t=TILES, u=2)
+        adj_words = adj_twice[:].rearrange("p t e -> p (t e)").bitcast(F32)
+        w_grouped_words = w_grouped[:].bitcast(F32)
+
+        def lay_out_atoms(rnd):
+            nc.vector.tensor_copy(
+                out=features[:, rnd * ROUND : (rnd + 1) * ROUND, :, 0:ATOM_K],
+                in_=atom_words.unsqueeze(1).to_broadcast([P, ROUND, 2, ATOM_K]),
+            )
+
+        def spread_adj(rnd):
+            adj_bank = adj_psum.tile([P, ROUND, P], F32)
+            for i in range(ROUND):
+                t = rnd * ROUND + i
+                nc.tensor.transpose(
+                    adj_bank[:, i, :], adj_words[:, t : t + 1].to_broadcast([P, P]), identity[:]
+                )
+            nc.scalar.copy(out=adj_spread[:, rnd * ROUND : (rnd + 1) * ROUND, :], in_=adj_bank[:])
+
+        def turn(step):
+            turned = turn_psum.tile([P, 2, BANK_TILES, P], F32)
+            for i in range(BANK_TILES):
+                for u in range(2):
+                    nc.tensor.transpose(
+                        turned[:, u, i, :], features[:, step * BANK_TILES + i, u, :], identity[:]
+                    )
+            return turned
+
+        def gate(step, turned):
+            both = slice(step * BANK_TILES, (step + 1) * BANK_TILES)
+            nc.vector.tensor_tensor(
+                out=g_grouped[:, both, :].rearrange("p t (c u e) -> p (t c) u e", u=2, e=2),
+                in0=turned[:].bitcast(BF16).rearrange("p u t (c e) -> p (t c) u e", e=2),
+                in1=adj_spread[:, both, :]
+                .bitcast(BF16)
+                .rearrange("p t (c e) -> p (t c) e", e=2)
+                .unsqueeze(2)
+                .to_broadcast([P, BANK_TILES * P, 2, 2]),
+                op=mybir.AluOpType.mult,
+            )
+
+        def quantise_pairs(step):
+            both = slice(step * BANK_TILES, (step + 1) * BANK_TILES)
+            columns = slice(step * BANK_TILES * P, (step + 1) * BANK_TILES * P)
+            nc.vector.quantize_mx(
+                out=g_codes[:, columns].bitcast(FP8X4),
+                scales=g_scales[:, columns],
+                in_=g_grouped[:, both, :].rearrange("p t c -> p (t c)"),
+            )
+
+        def quantise_weights(g):
+            turned = acc_psum.tile([P, 2, 2, P], F32, tag="acc")
+            for r in range(2):
+                words = w_sb[:, g, r, :].bitcast(F32).rearrange("p (k u) -> p u k", u=2)
+                for u in range(2):
+                    nc.tensor.transpose(turned[:, r, u, :], words[:, u, :], identity[:])
+            nc.scalar.copy(
+                out=w_grouped_words[:, g * W_GROUP_H * 2 : (g + 1) * W_GROUP_H * 2].rearrange(
+                    "k (p w) -> k p w", w=4
+                ),
+                in_=turned[:].rearrange("k r u p -> k p (r u)"),
+            )
+            h_rows = slice(g * W_GROUP_H, (g + 1) * W_GROUP_H)
+            nc.vector.quantize_mx(
+                out=w_codes[:, h_rows].bitcast(FP8X4),
+                scales=w_scales[:, h_rows],
+                in_=w_grouped[:, g * W_GROUP_H * PACK : (g + 1) * W_GROUP_H * PACK],
+            )
+
+        def project(step):
+            result = results.tile([P, BANK_TILES, H], F32)
+            for i in range(BANK_TILES):
+                t = step * BANK_TILES + i
+                pairs = slice(t * P, (t + 1) * P)
+                for half in range(H // N_PASS):
+                    h_cols = slice(half * N_PASS, (half + 1) * N_PASS)
+                    acc = acc_psum.tile([P, N_PASS], F32, tag="acc")
+                    nc.tensor.matmul_mx(
+                        out=acc[:],
+                        lhsT=g_codes[:, pairs].bitcast(FP8X4),
+                        lhsT_scale=g_scales[:, pairs],
+                        rhs=w_codes[:, h_cols].bitcast(FP8X4),
+                        rhs_scale=w_scales[:, h_cols],
+                        start=True,
+                        stop=True,
+                    )
+                    if i == 0 and half == 1:
+                        nc.vector.tensor_copy(out=result[:, i, h_cols], in_=acc[:])
+                    else:
+                        nc.scalar.copy(out=result[:, i, h_cols], in_=acc[:])
+            first = step * BANK_TILES
+            nc.sync.dma_start(out=out_rows[:, first : first + BANK_TILES, :], in_=result[:])
+
+        nc.vector.tensor_copy(
+            out=adj_twice[:], in_=adj_cols[:].unsqueeze(2).to_broadcast([P, TILES, 2])
+        )
+        nc.vector.tensor_copy(
+            out=features[:, :, :, ATOM_K:P].rearrange("p t u (c k) -> p t u c k", c=2),
+            in_=bond_words.unsqueeze(3).to_broadcast([P, TILES, 2, 2, BOND_K]),
+        )
+        lay_out_atoms(0)
+        spread_adj(0)
+        turned_ahead = [turn(0), turn(1)]
+        for g in range(W_GROUPS):
+            if g % 2 == 0:
+                gate(g // 2, turned_ahead[g // 2])
+            else:
+                quantise_pairs(g // 2)
+            quantise_weights(g)
+        lay_out_atoms(1)
+        spread_adj(1)
+
+        for step in range(STEPS):
+            ahead = step + AHEAD
+            if ahead < STEPS:
+                turned = turn(ahead)
+            project(step)
+            if ahead < STEPS:
+                gate(ahead, turned)
+                quantise_pairs(ahead)
+            later = (ahead + AHEAD) // 2
+            if step % 2 == 0 and later < TILES // ROUND:
+                lay_out_atoms(later)
+                spread_adj(later)

@@ -146,12 +146,12 @@ def tile_mpnencoder_pa_kernel(tc, f_atoms, f_bonds, adj, W_i_w, out):
             )
 
         def project(step):
+            first = step * BANK_TILES
             result = results.tile([P, BANK_TILES, H], F32)
-            for i in range(BANK_TILES):
-                t = step * BANK_TILES + i
-                pairs = slice(t * P, (t + 1) * P)
-                for half in range(H // N_PASS):
-                    h_cols = slice(half * N_PASS, (half + 1) * N_PASS)
+            for half in range(H // N_PASS):
+                h_cols = slice(half * N_PASS, (half + 1) * N_PASS)
+                for i in range(BANK_TILES):
+                    pairs = slice((first + i) * P, (first + i + 1) * P)
                     acc = acc_psum.tile([P, N_PASS], F32, tag="acc")
                     nc.tensor.matmul_mx(
                         out=acc[:],
@@ -162,12 +162,16 @@ def tile_mpnencoder_pa_kernel(tc, f_atoms, f_bonds, adj, W_i_w, out):
                         start=True,
                         stop=True,
                     )
-                    if i == 0 and half == 1:
+                    bank = (step * (H // N_PASS) + half) * BANK_TILES + i
+                    if bank % 3 == 1:
                         nc.vector.tensor_copy(out=result[:, i, h_cols], in_=acc[:])
                     else:
                         nc.scalar.copy(out=result[:, i, h_cols], in_=acc[:])
-            first = step * BANK_TILES
-            nc.sync.dma_start(out=out_rows[:, first : first + BANK_TILES, :], in_=result[:])
+            if step == 0 or step == STEPS - 1:
+                for i in range(BANK_TILES):
+                    nc.sync.dma_start(out=out_rows[:, first + i, :], in_=result[:, i, :])
+            else:
+                nc.sync.dma_start(out=out_rows[:, first : first + BANK_TILES, :], in_=result[:])
 
         nc.vector.tensor_copy(
             out=adj_twice[:], in_=adj_cols[:].unsqueeze(2).to_broadcast([P, TILES, 2])
@@ -178,25 +182,27 @@ def tile_mpnencoder_pa_kernel(tc, f_atoms, f_bonds, adj, W_i_w, out):
         )
         lay_out_atoms(0)
         spread_adj(0)
-        turned_ahead = [turn(0), turn(1)]
-        for g in range(W_GROUPS):
-            if g % 2 == 0:
-                gate(g // 2, turned_ahead[g // 2])
-            else:
-                quantise_pairs(g // 2)
-            quantise_weights(g)
+        turned = turn(0)
+        gate(0, turned)
+        quantise_weights(0)
+        quantise_pairs(0)
+        quantise_weights(1)
         lay_out_atoms(1)
+        quantise_weights(2)
+        quantise_weights(3)
+        turned = turn(1)
+        gate(1, turned)
+        quantise_pairs(1)
         spread_adj(1)
 
         for step in range(STEPS):
+            project(step)
             ahead = step + AHEAD
             if ahead < STEPS:
                 turned = turn(ahead)
-            project(step)
-            if ahead < STEPS:
                 gate(ahead, turned)
                 quantise_pairs(ahead)
-            later = (ahead + AHEAD) // 2
-            if step % 2 == 0 and later < TILES // ROUND:
-                lay_out_atoms(later)
-                spread_adj(later)
+            rnd = (ahead + 1) // 2
+            if step % 2 == 1 and rnd < TILES // ROUND:
+                lay_out_atoms(rnd)
+                spread_adj(rnd)

@@ -18,15 +18,16 @@ ATOM_COLS = ATOM_F + (ATOM_F - TAIL_START)
 BOND_F = 32
 F = ATOM_COLS + 2 * BOND_F
 H = 1024
-ATOM_K = ATOM_COLS // PACK
+ATOM_K = ATOM_F // PACK
+TAIL_K = TAIL_START // PACK
+ATOMS_K = ATOM_COLS // PACK
 BOND_K = BOND_F // PACK
 N_PASS = 512
 W_GROUPS = 4
 W_GROUP_H = H // W_GROUPS
-ROUND = 4
-BANK_TILES = 2
-STEPS = TILES // BANK_TILES
-AHEAD = 2
+STEP_TILES = 2
+STEPS = TILES // STEP_TILES
+STEP_WORDS = STEP_TILES * P * 2
 
 FLOPS = 2 * P * TILES * F * H
 
@@ -42,33 +43,34 @@ def tile_mpnencoder_pa_kernel(tc, f_atoms, f_bonds, adj, W_i_w, out):
 
     with ExitStack() as ctx:
         keep = ctx.enter_context(tc.tile_pool(name="keep", bufs=1))
-        results = ctx.enter_context(tc.tile_pool(name="results", bufs=4))
-        adj_psum = ctx.enter_context(tc.psum_pool(name="adj_psum", bufs=1))
+        results = ctx.enter_context(tc.tile_pool(name="results", bufs=TILES))
         turn_psum = ctx.enter_context(tc.psum_pool(name="turn_psum", bufs=2))
-        acc_psum = ctx.enter_context(tc.psum_pool(name="acc_psum", bufs=5))
+        acc_psum = ctx.enter_context(tc.psum_pool(name="acc_psum", bufs=6))
         ctx.enter_context(tc.manual_schedule())
 
         adj_cols = keep.tile([P, TILES], BF16)
-        nc.scalar.dma_start(out=adj_cols[:], in_=adj_rows)
-        atoms = keep.tile([P, ATOM_COLS], BF16)
-        for s in range(2):
-            nc.scalar.dma_start(out=atoms[s:P:2, 0:ATOM_F], in_=atom_rows)
-            nc.scalar.dma_start(
-                out=atoms[s:P:2, ATOM_F:ATOM_COLS], in_=atom_rows[:, TAIL_START:ATOM_F]
-            )
+        atoms = keep.tile([P, ATOM_F], BF16)
         bonds = keep.tile([P, TILES * BOND_F], BF16)
-        nc.scalar.dma_start(out=bonds[:], in_=bond_rows)
         w_sb = keep.tile([P, W_GROUPS, 2, F], BF16)
-        for g in range(W_GROUPS):
+
+        def load_weights(g):
             nc.sync.dma_start(out=w_sb[:, g].rearrange("p r f -> p (r f)"), in_=w_rows[g])
+
+        nc.sync.dma_start(out=adj_cols[:], in_=adj_rows)
+        for s in range(2):
+            nc.sync.dma_start(out=atoms[s:P:2, :], in_=atom_rows)
+        load_weights(0)
+        nc.sync.dma_start(out=bonds[:], in_=bond_rows)
+        for g in range(1, W_GROUPS):
+            load_weights(g)
 
         identity = keep.tile([P, P], F32)
         make_identity(nc, identity[:])
 
-        features = keep.tile([P, TILES, 2, P], F32)
-        adj_twice = keep.tile([P, TILES, 2], BF16)
-        adj_spread = keep.tile([P, TILES, P], F32)
-        g_grouped = keep.tile([P, TILES, P * PACK], BF16, align_bytes=64)
+        atoms_sorted = keep.tile([P, 2, ATOMS_K], F32)
+        bonds_sorted = keep.tile([P, TILES, 2, BOND_K], F32)
+        g_rows = keep.tile([P, TILES, 2, P * 2], BF16)
+        g_grouped = keep.tile([P, TILES * P * PACK], BF16, align_bytes=64)
         g_codes = keep.tile([P, TILES * P], U32, align_bytes=64)
         g_scales = keep.tile([P, TILES * P], U8, align_bytes=64)
         w_grouped = keep.tile([P, H * PACK], BF16, align_bytes=64)
@@ -77,56 +79,77 @@ def tile_mpnencoder_pa_kernel(tc, f_atoms, f_bonds, adj, W_i_w, out):
 
         atom_words = atoms[:].bitcast(F32).rearrange("p (k u) -> p u k", u=2)
         bond_words = bonds[:].bitcast(F32).rearrange("p (t k u) -> p t u k", t=TILES, u=2)
-        adj_words = adj_twice[:].rearrange("p t e -> p (t e)").bitcast(F32)
+        atoms_by_u = (
+            atoms_sorted[:]
+            .rearrange("p u k -> p (u k)")
+            .bitcast(BF16)
+            .rearrange("p (u w) -> p u w", u=2)
+        )
+        bonds_by_u = (
+            bonds_sorted[:]
+            .rearrange("p t u k -> p (t u k)")
+            .bitcast(BF16)
+            .rearrange("p (t u w) -> p t u w", t=TILES, u=2)
+        )
+        g_row_words = (
+            g_rows[:]
+            .rearrange("p t u w -> p (t u w)")
+            .bitcast(F32)
+            .rearrange("p (t u k) -> p t u k", t=TILES, u=2)
+        )
+        g_grouped_words = g_grouped[:].bitcast(F32)
         w_grouped_words = w_grouped[:].bitcast(F32)
 
-        def lay_out_atoms(rnd):
+        def sort_bonds(first, last):
             nc.vector.tensor_copy(
-                out=features[:, rnd * ROUND : (rnd + 1) * ROUND, :, 0:ATOM_K],
-                in_=atom_words.unsqueeze(1).to_broadcast([P, ROUND, 2, ATOM_K]),
+                out=bonds_sorted[:, first:last], in_=bond_words[:, first:last]
             )
 
-        def spread_adj(rnd):
-            adj_bank = adj_psum.tile([P, ROUND, P], F32)
-            for i in range(ROUND):
-                t = rnd * ROUND + i
-                nc.tensor.transpose(
-                    adj_bank[:, i, :], adj_words[:, t : t + 1].to_broadcast([P, P]), identity[:]
-                )
-            nc.scalar.copy(out=adj_spread[:, rnd * ROUND : (rnd + 1) * ROUND, :], in_=adj_bank[:])
+        def gate_atoms(t):
+            nc.vector.tensor_scalar_mul(
+                out=g_rows[:, t, :, 0 : ATOMS_K * 2],
+                in0=atoms_by_u,
+                scalar1=adj_cols[:, t : t + 1],
+            )
+
+        def gate_bonds(t):
+            nc.vector.tensor_scalar_mul(
+                out=g_rows[:, t, :, ATOMS_K * 2 :].rearrange("p u (c w) -> p u c w", c=2),
+                in0=bonds_by_u[:, t].unsqueeze(2).to_broadcast([P, 2, 2, BOND_K * 2]),
+                scalar1=adj_cols[:, t : t + 1],
+            )
+
+        def gate(step):
+            for i in range(STEP_TILES):
+                gate_atoms(step * STEP_TILES + i)
+                gate_bonds(step * STEP_TILES + i)
 
         def turn(step):
-            turned = turn_psum.tile([P, 2, BANK_TILES, P], F32)
-            for i in range(BANK_TILES):
+            turned = turn_psum.tile([P, STEP_TILES, 2, P], F32)
+            for i in range(STEP_TILES):
                 for u in range(2):
                     nc.tensor.transpose(
-                        turned[:, u, i, :], features[:, step * BANK_TILES + i, u, :], identity[:]
+                        turned[:, i, u, :], g_row_words[:, step * STEP_TILES + i, u, :], identity[:]
                     )
             return turned
 
-        def gate(step, turned):
-            both = slice(step * BANK_TILES, (step + 1) * BANK_TILES)
-            nc.vector.tensor_tensor(
-                out=g_grouped[:, both, :].rearrange("p t (c u e) -> p (t c) u e", u=2, e=2),
-                in0=turned[:].bitcast(BF16).rearrange("p u t (c e) -> p (t c) u e", e=2),
-                in1=adj_spread[:, both, :]
-                .bitcast(BF16)
-                .rearrange("p t (c e) -> p (t c) e", e=2)
-                .unsqueeze(2)
-                .to_broadcast([P, BANK_TILES * P, 2, 2]),
-                op=mybir.AluOpType.mult,
+        def collect(copy, step, turned):
+            copy(
+                out=g_grouped_words[:, step * STEP_WORDS : (step + 1) * STEP_WORDS].rearrange(
+                    "k (i c u) -> k i c u", i=STEP_TILES, u=2
+                ),
+                in_=turned[:].rearrange("k i u c -> k i c u"),
             )
 
         def quantise_pairs(step):
-            both = slice(step * BANK_TILES, (step + 1) * BANK_TILES)
-            columns = slice(step * BANK_TILES * P, (step + 1) * BANK_TILES * P)
+            columns = slice(step * STEP_TILES * P, (step + 1) * STEP_TILES * P)
             nc.vector.quantize_mx(
                 out=g_codes[:, columns].bitcast(FP8X4),
                 scales=g_scales[:, columns],
-                in_=g_grouped[:, both, :].rearrange("p t c -> p (t c)"),
+                in_=g_grouped[:, step * STEP_WORDS * 2 : (step + 1) * STEP_WORDS * 2],
             )
 
-        def quantise_weights(g):
+        def turn_weights(g):
             turned = acc_psum.tile([P, 2, 2, P], F32, tag="acc")
             for r in range(2):
                 words = w_sb[:, g, r, :].bitcast(F32).rearrange("p (k u) -> p u k", u=2)
@@ -138,6 +161,8 @@ def tile_mpnencoder_pa_kernel(tc, f_atoms, f_bonds, adj, W_i_w, out):
                 ),
                 in_=turned[:].rearrange("k r u p -> k p (r u)"),
             )
+
+        def quantise_weights(g):
             h_rows = slice(g * W_GROUP_H, (g + 1) * W_GROUP_H)
             nc.vector.quantize_mx(
                 out=w_codes[:, h_rows].bitcast(FP8X4),
@@ -145,64 +170,80 @@ def tile_mpnencoder_pa_kernel(tc, f_atoms, f_bonds, adj, W_i_w, out):
                 in_=w_grouped[:, g * W_GROUP_H * PACK : (g + 1) * W_GROUP_H * PACK],
             )
 
-        def project(step):
-            first = step * BANK_TILES
-            result = results.tile([P, BANK_TILES, H], F32)
-            for half in range(H // N_PASS):
-                h_cols = slice(half * N_PASS, (half + 1) * N_PASS)
-                for i in range(BANK_TILES):
-                    pairs = slice((first + i) * P, (first + i + 1) * P)
-                    acc = acc_psum.tile([P, N_PASS], F32, tag="acc")
-                    nc.tensor.matmul_mx(
-                        out=acc[:],
-                        lhsT=g_codes[:, pairs].bitcast(FP8X4),
-                        lhsT_scale=g_scales[:, pairs],
-                        rhs=w_codes[:, h_cols].bitcast(FP8X4),
-                        rhs_scale=w_scales[:, h_cols],
-                        start=True,
-                        stop=True,
-                    )
-                    bank = (step * (H // N_PASS) + half) * BANK_TILES + i
-                    if bank % 3 == 1:
-                        nc.vector.tensor_copy(out=result[:, i, h_cols], in_=acc[:])
-                    else:
-                        nc.scalar.copy(out=result[:, i, h_cols], in_=acc[:])
-            if step == 0 or step == STEPS - 1:
-                for i in range(BANK_TILES):
-                    nc.sync.dma_start(out=out_rows[:, first + i, :], in_=result[:, i, :])
-            else:
-                nc.sync.dma_start(out=out_rows[:, first : first + BANK_TILES, :], in_=result[:])
+        def multiply(t, half):
+            pairs = slice(t * P, (t + 1) * P)
+            h_cols = slice(half * N_PASS, (half + 1) * N_PASS)
+            acc = acc_psum.tile([P, N_PASS], F32, tag="acc")
+            nc.tensor.matmul_mx(
+                out=acc[:],
+                lhsT=g_codes[:, pairs].bitcast(FP8X4),
+                lhsT_scale=g_scales[:, pairs],
+                rhs=w_codes[:, h_cols].bitcast(FP8X4),
+                rhs_scale=w_scales[:, h_cols],
+                start=True,
+                stop=True,
+            )
+            return acc
 
+        def half_of(result, half):
+            return result[:, half * N_PASS : (half + 1) * N_PASS]
+
+        nc.vector.tensor_copy(out=atoms_sorted[:, :, 0:ATOM_K], in_=atom_words)
         nc.vector.tensor_copy(
-            out=adj_twice[:], in_=adj_cols[:].unsqueeze(2).to_broadcast([P, TILES, 2])
+            out=atoms_sorted[:, :, ATOM_K:ATOMS_K], in_=atom_words[:, :, TAIL_K:ATOM_K]
         )
-        nc.vector.tensor_copy(
-            out=features[:, :, :, ATOM_K:P].rearrange("p t u (c k) -> p t u c k", c=2),
-            in_=bond_words.unsqueeze(3).to_broadcast([P, TILES, 2, 2, BOND_K]),
-        )
-        lay_out_atoms(0)
-        spread_adj(0)
+        gate_atoms(0)
+        gate_atoms(1)
+        sort_bonds(0, 4)
+        gate_bonds(0)
+        gate_bonds(1)
+        turn_weights(0)
         turned = turn(0)
-        gate(0, turned)
+        collect(nc.scalar.copy, 0, turned)
+        turn_weights(1)
         quantise_weights(0)
+        sort_bonds(4, TILES)
         quantise_pairs(0)
+        gate(1)
         quantise_weights(1)
-        lay_out_atoms(1)
+        turn_weights(2)
         quantise_weights(2)
-        quantise_weights(3)
-        turned = turn(1)
-        gate(1, turned)
-        quantise_pairs(1)
-        spread_adj(1)
+        turn_weights(3)
 
-        for step in range(STEPS):
-            project(step)
-            ahead = step + AHEAD
-            if ahead < STEPS:
-                turned = turn(ahead)
-                gate(ahead, turned)
-                quantise_pairs(ahead)
-            rnd = (ahead + 1) // 2
-            if step % 2 == 1 and rnd < TILES // ROUND:
-                lay_out_atoms(rnd)
-                spread_adj(rnd)
+        first = [results.tile([P, H], F32, name="result") for t in range(STEP_TILES)]
+        for half in range(H // N_PASS):
+            for t in range(STEP_TILES):
+                acc = multiply(t, half)
+                copy = nc.vector.tensor_copy if t == 0 else nc.scalar.copy
+                copy(out=half_of(first[t], half), in_=acc[:])
+                nc.sync.dma_start(
+                    out=out_rows[:, t, half * N_PASS : (half + 1) * N_PASS],
+                    in_=half_of(first[t], half),
+                )
+                if t == 0 and half == 0:
+                    quantise_weights(3)
+                    gate(2)
+            if half == 0:
+                turned = turn(1)
+                collect(nc.scalar.copy, 1, turned)
+        quantise_pairs(1)
+        turned = turn(2)
+        gate(3)
+
+        for step in range(1, STEPS):
+            if step + 1 < STEPS:
+                collect(nc.scalar.copy, step + 1, turned)
+            for i in range(STEP_TILES):
+                t = step * STEP_TILES + i
+                result = results.tile([P, H], F32, name="result")
+                acc = multiply(t, 0)
+                nc.vector.tensor_copy(out=half_of(result, 0), in_=acc[:])
+                acc = multiply(t, 1)
+                nc.scalar.copy(out=half_of(result, 1), in_=acc[:])
+                nc.sync.dma_start(out=out_rows[:, t, :], in_=result[:])
+                if i == 0 and step + 1 < STEPS:
+                    quantise_pairs(step + 1)
+            if step + 2 < STEPS:
+                turned = turn(step + 2)
+            if step + 3 < STEPS:
+                gate(step + 3)

@@ -43,7 +43,7 @@ def tile_mpnencoder_pa_kernel(tc, f_atoms, f_bonds, adj, W_i_w, out):
 
     with ExitStack() as ctx:
         keep = ctx.enter_context(tc.tile_pool(name="keep", bufs=1))
-        results = ctx.enter_context(tc.tile_pool(name="results", bufs=TILES))
+        results = ctx.enter_context(tc.tile_pool(name="results", bufs=STEPS))
         turn_psum = ctx.enter_context(tc.psum_pool(name="turn_psum", bufs=2))
         acc_psum = ctx.enter_context(tc.psum_pool(name="acc_psum", bufs=6))
         ctx.enter_context(tc.manual_schedule())
@@ -210,15 +210,15 @@ def tile_mpnencoder_pa_kernel(tc, f_atoms, f_bonds, adj, W_i_w, out):
         quantise_weights(2)
         turn_weights(3)
 
-        first = [results.tile([P, H], F32, name="result") for t in range(STEP_TILES)]
+        first = results.tile([P, STEP_TILES, H], F32, name="result")
         for half in range(H // N_PASS):
             for t in range(STEP_TILES):
                 acc = multiply(t, half)
                 copy = nc.vector.tensor_copy if t == 0 else nc.scalar.copy
-                copy(out=half_of(first[t], half), in_=acc[:])
+                copy(out=half_of(first[:, t], half), in_=acc[:])
                 nc.sync.dma_start(
                     out=out_rows[:, t, half * N_PASS : (half + 1) * N_PASS],
-                    in_=half_of(first[t], half),
+                    in_=half_of(first[:, t], half),
                 )
                 if t == 0 and half == 0:
                     quantise_weights(3)
@@ -233,16 +233,21 @@ def tile_mpnencoder_pa_kernel(tc, f_atoms, f_bonds, adj, W_i_w, out):
         for step in range(1, STEPS):
             if step + 1 < STEPS:
                 collect(nc.scalar.copy, step + 1, turned)
+            result = results.tile([P, STEP_TILES, H], F32, name="result")
             for i in range(STEP_TILES):
                 t = step * STEP_TILES + i
-                result = results.tile([P, H], F32, name="result")
                 acc = multiply(t, 0)
-                nc.vector.tensor_copy(out=half_of(result, 0), in_=acc[:])
+                nc.vector.tensor_copy(out=half_of(result[:, i], 0), in_=acc[:])
                 acc = multiply(t, 1)
-                nc.scalar.copy(out=half_of(result, 1), in_=acc[:])
-                nc.sync.dma_start(out=out_rows[:, t, :], in_=result[:])
+                nc.scalar.copy(out=half_of(result[:, i], 1), in_=acc[:])
+                if step < 3:
+                    nc.sync.dma_start(out=out_rows[:, t, :], in_=result[:, i])
                 if i == 0 and step + 1 < STEPS:
                     quantise_pairs(step + 1)
+            if step >= 3:
+                nc.sync.dma_start(
+                    out=out_rows[:, step * STEP_TILES : (step + 1) * STEP_TILES, :], in_=result[:]
+                )
             if step + 2 < STEPS:
                 turned = turn(step + 2)
             if step + 3 < STEPS:

@@ -188,6 +188,17 @@ def tile_mpnencoder_pa_kernel(tc, f_atoms, f_bonds, adj, W_i_w, out):
         def half_of(result, half):
             return result[:, half * N_PASS : (half + 1) * N_PASS]
 
+        zeros = keep.tile([P, P], BF16)
+        nc.vector.memset(zeros[:], 0.0)
+        warm = acc_psum.tile([P, 4, P], F32, tag="acc")
+        for i in range(4):
+            nc.tensor.matmul(
+                warm[:],
+                lhsT=zeros[:],
+                rhs=zeros[:].unsqueeze(1).to_broadcast([P, 4, P]),
+                start=True,
+                stop=True,
+            )
         nc.vector.tensor_copy(out=atoms_sorted[:, :, 0:ATOM_K], in_=atom_words)
         nc.vector.tensor_copy(
             out=atoms_sorted[:, :, ATOM_K:ATOMS_K], in_=atom_words[:, :, TAIL_K:ATOM_K]

@@ -68,7 +68,7 @@ def tile_mpnencoder_pa_kernel(tc, f_atoms, f_bonds, adj, W_i_w, out):
         make_identity(nc, identity[:])
 
         atoms_sorted = keep.tile([P, 2, ATOMS_K], F32)
-        bonds_sorted = keep.tile([P, TILES, 2, BOND_K], F32)
+        adj_twice = keep.tile([P, TILES, 2], BF16)
         g_rows = keep.tile([P, TILES, 2, P * 2], BF16)
         g_grouped = keep.tile([P, TILES * P * PACK], BF16, align_bytes=64)
         g_codes = keep.tile([P, TILES * P], U32, align_bytes=64)
@@ -78,19 +78,13 @@ def tile_mpnencoder_pa_kernel(tc, f_atoms, f_bonds, adj, W_i_w, out):
         w_scales = keep.tile([P, H], U8, align_bytes=64)
 
         atom_words = atoms[:].bitcast(F32).rearrange("p (k u) -> p u k", u=2)
-        bond_words = bonds[:].bitcast(F32).rearrange("p (t k u) -> p t u k", t=TILES, u=2)
         atoms_by_u = (
             atoms_sorted[:]
             .rearrange("p u k -> p (u k)")
             .bitcast(BF16)
             .rearrange("p (u w) -> p u w", u=2)
         )
-        bonds_by_u = (
-            bonds_sorted[:]
-            .rearrange("p t u k -> p (t u k)")
-            .bitcast(BF16)
-            .rearrange("p (t u w) -> p t u w", t=TILES, u=2)
-        )
+        bonds_by_u = bonds[:].rearrange("p (t k u e) -> p t u k e", t=TILES, u=2, e=2)
         g_row_words = (
             g_rows[:]
             .rearrange("p t u w -> p (t u w)")
@@ -100,11 +94,6 @@ def tile_mpnencoder_pa_kernel(tc, f_atoms, f_bonds, adj, W_i_w, out):
         g_grouped_words = g_grouped[:].bitcast(F32)
         w_grouped_words = w_grouped[:].bitcast(F32)
 
-        def sort_bonds(first, last):
-            nc.vector.tensor_copy(
-                out=bonds_sorted[:, first:last], in_=bond_words[:, first:last]
-            )
-
         def gate_atoms(t):
             nc.vector.tensor_scalar_mul(
                 out=g_rows[:, t, :, 0 : ATOMS_K * 2],
@@ -112,20 +101,24 @@ def tile_mpnencoder_pa_kernel(tc, f_atoms, f_bonds, adj, W_i_w, out):
                 scalar1=adj_cols[:, t : t + 1],
             )
 
-        def gate_bonds(t):
-            nc.vector.tensor_scalar_mul(
-                out=g_rows[:, t, :, ATOMS_K * 2 :].rearrange("p u (c w) -> p u c w", c=2),
-                in0=bonds_by_u[:, t].unsqueeze(2).to_broadcast([P, 2, 2, BOND_K * 2]),
-                scalar1=adj_cols[:, t : t + 1],
-            )
-
-        def gate(step):
-            for i in range(STEP_TILES):
-                gate_atoms(step * STEP_TILES + i)
-                gate_bonds(step * STEP_TILES + i)
+        def gate_bonds(first, last):
+            tiles = slice(first, last)
+            for u in range(2):
+                for c in range(2):
+                    start = (ATOMS_K + c * BOND_K) * 2
+                    nc.vector.tensor_tensor(
+                        out=g_rows[:, tiles, u, start : start + BOND_K * 2].rearrange(
+                            "p t (k e) -> p t k e", e=2
+                        ),
+                        in0=bonds_by_u[:, tiles, u],
+                        in1=adj_twice[:, tiles]
+                        .unsqueeze(2)
+                        .to_broadcast([P, last - first, BOND_K, 2]),
+                        op=mybir.AluOpType.mult,
+                    )
 
         def turn(step):
-            turned = turn_psum.tile([P, STEP_TILES, 2, P], F32)
+            turned = turn_psum.tile([P, STEP_TILES, 2, P], F32, tag="turned")
             for i in range(STEP_TILES):
                 for u in range(2):
                     nc.tensor.transpose(
@@ -188,6 +181,27 @@ def tile_mpnencoder_pa_kernel(tc, f_atoms, f_bonds, adj, W_i_w, out):
         def half_of(result, half):
             return result[:, half * N_PASS : (half + 1) * N_PASS]
 
+        def turn_tile(t):
+            turned = turn_psum.tile([P, 2, P], F32, tag="turned")
+            for u in range(2):
+                nc.tensor.transpose(turned[:, u, :], g_row_words[:, t, u, :], identity[:])
+            return turned
+
+        def collect_tile(t, turned):
+            nc.vector.tensor_copy(
+                out=g_grouped_words[:, t * P * 2 : (t + 1) * P * 2].rearrange(
+                    "k (c u) -> k c u", u=2
+                ),
+                in_=turned[:].rearrange("k u c -> k c u"),
+            )
+
+        def quantise_tile(t):
+            nc.vector.quantize_mx(
+                out=g_codes[:, t * P : (t + 1) * P].bitcast(FP8X4),
+                scales=g_scales[:, t * P : (t + 1) * P],
+                in_=g_grouped[:, t * P * PACK : (t + 1) * P * PACK],
+            )
+
         zeros = keep.tile([P, P], BF16)
         nc.vector.memset(zeros[:], 0.0)
         warm = acc_psum.tile([P, 4, P], F32, tag="acc")
@@ -199,67 +213,86 @@ def tile_mpnencoder_pa_kernel(tc, f_atoms, f_bonds, adj, W_i_w, out):
                 start=True,
                 stop=True,
             )
+        nc.vector.tensor_copy(
+            out=adj_twice[:], in_=adj_cols[:].unsqueeze(2).to_broadcast([P, TILES, 2])
+        )
         nc.vector.tensor_copy(out=atoms_sorted[:, :, 0:ATOM_K], in_=atom_words)
         nc.vector.tensor_copy(
             out=atoms_sorted[:, :, ATOM_K:ATOMS_K], in_=atom_words[:, :, TAIL_K:ATOM_K]
         )
         gate_atoms(0)
         gate_atoms(1)
-        sort_bonds(0, 4)
-        gate_bonds(0)
-        gate_bonds(1)
+        gate_bonds(0, 6)
         turn_weights(0)
-        turned = turn(0)
-        collect(nc.scalar.copy, 0, turned)
+        turned_0 = turn_tile(0)
         turn_weights(1)
+        turned_1 = turn_tile(1)
+        for t in range(2, 6):
+            gate_atoms(t)
+        collect_tile(0, turned_0)
         quantise_weights(0)
-        sort_bonds(4, TILES)
-        quantise_pairs(0)
-        gate(1)
+        quantise_tile(0)
+        collect_tile(1, turned_1)
         quantise_weights(1)
+        quantise_tile(1)
         turn_weights(2)
-        quantise_weights(2)
         turn_weights(3)
+        quantise_weights(2)
+        quantise_weights(3)
+        turned = turn(1)
+        collect(nc.vector.tensor_copy, 1, turned)
 
         first = results.tile([P, STEP_TILES, H], F32, name="result")
-        for half in range(H // N_PASS):
-            for t in range(STEP_TILES):
-                acc = multiply(t, half)
-                copy = nc.vector.tensor_copy if t == 0 else nc.scalar.copy
-                copy(out=half_of(first[:, t], half), in_=acc[:])
-                nc.sync.dma_start(
-                    out=out_rows[:, t, half * N_PASS : (half + 1) * N_PASS],
-                    in_=half_of(first[:, t], half),
-                )
-                if t == 0 and half == 0:
-                    quantise_weights(3)
-                    gate(2)
-            if half == 0:
-                turned = turn(1)
-                collect(nc.scalar.copy, 1, turned)
-        quantise_pairs(1)
+
+        def leave(t, half, acc):
+            nc.scalar.copy(out=half_of(first[:, t], half), in_=acc[:])
+            nc.sync.dma_start(
+                out=out_rows[:, t, half * N_PASS : (half + 1) * N_PASS],
+                in_=half_of(first[:, t], half),
+            )
+
+        acc_0 = multiply(0, 0)
+        acc_1 = multiply(1, 0)
         turned = turn(2)
-        gate(3)
+        leave(0, 0, acc_0)
+        leave(1, 0, acc_1)
+        quantise_pairs(1)
+        collect(nc.vector.tensor_copy, 2, turned)
+        acc_0 = multiply(0, 1)
+        acc_1 = multiply(1, 1)
+        leave(0, 1, acc_0)
+        leave(1, 1, acc_1)
 
         for step in range(1, STEPS):
-            if step + 1 < STEPS:
-                collect(nc.scalar.copy, step + 1, turned)
             result = results.tile([P, STEP_TILES, H], F32, name="result")
+            if step > 2 and step + 1 < STEPS:
+                collect(nc.scalar.copy, step + 1, turned)
             for i in range(STEP_TILES):
                 t = step * STEP_TILES + i
                 acc = multiply(t, 0)
                 nc.vector.tensor_copy(out=half_of(result[:, i], 0), in_=acc[:])
                 acc = multiply(t, 1)
                 nc.scalar.copy(out=half_of(result[:, i], 1), in_=acc[:])
-                if step < 3:
+                if step <= 3:
                     nc.sync.dma_start(out=out_rows[:, t, :], in_=result[:, i])
-                if i == 0 and step + 1 < STEPS:
+                if step == 2 and i == 0:
+                    turned = turn(3)
+                    collect(nc.scalar.copy, 3, turned)
+                if i == (1 if step == 2 else 0) and step + 1 < STEPS:
                     quantise_pairs(step + 1)
-            if step >= 3:
+                if i == 0 and step == 1:
+                    gate_bonds(6, TILES)
+                    gate_atoms(6)
+                    gate_atoms(7)
+                if i == 0 and step == 2:
+                    gate_atoms(8)
+                    gate_atoms(9)
+            if step > 3:
                 nc.sync.dma_start(
                     out=out_rows[:, step * STEP_TILES : (step + 1) * STEP_TILES, :], in_=result[:]
                 )
-            if step + 2 < STEPS:
+            if step > 1 and step + 2 < STEPS:
                 turned = turn(step + 2)
-            if step + 3 < STEPS:
-                gate(step + 3)
+            if step > 1 and step + 3 < STEPS:
+                gate_atoms((step + 3) * STEP_TILES)
+                gate_atoms((step + 3) * STEP_TILES + 1)

@@ -56,10 +56,14 @@ def tile_mpnencoder_pa_kernel(tc, f_atoms, f_bonds, adj, W_i_w, out):
         def load_weights(g):
             nc.sync.dma_start(out=w_sb[:, g].rearrange("p r f -> p (r f)"), in_=w_rows[g])
 
+        def load_first_weights(r):
+            nc.sync.dma_start(out=w_sb[:, 0, r], in_=W_i_w[r * P : (r + 1) * P, :])
+
+        load_first_weights(0)
         nc.sync.dma_start(out=adj_cols[:], in_=adj_rows)
         for s in range(2):
             nc.sync.dma_start(out=atoms[s:P:2, :], in_=atom_rows)
-        load_weights(0)
+        load_first_weights(1)
         nc.sync.dma_start(out=bonds[:], in_=bond_rows)
         for g in range(1, W_GROUPS):
             load_weights(g)
@@ -155,6 +159,18 @@ def tile_mpnencoder_pa_kernel(tc, f_atoms, f_bonds, adj, W_i_w, out):
                 in_=turned[:].rearrange("k r u p -> k p (r u)"),
             )
 
+        def turn_first_weights(r):
+            turned = acc_psum.tile([P, 2, P], F32, tag="acc")
+            words = w_sb[:, 0, r, :].bitcast(F32).rearrange("p (k u) -> p u k", u=2)
+            for u in range(2):
+                nc.tensor.transpose(turned[:, u, :], words[:, u, :], identity[:])
+            nc.scalar.copy(
+                out=w_grouped_words[:, r * P * 2 : (r + 1) * P * 2].rearrange(
+                    "k (p u) -> k p u", u=2
+                ),
+                in_=turned[:].rearrange("k u p -> k p u"),
+            )
+
         def quantise_weights(g):
             h_rows = slice(g * W_GROUP_H, (g + 1) * W_GROUP_H)
             nc.vector.quantize_mx(
@@ -187,8 +203,8 @@ def tile_mpnencoder_pa_kernel(tc, f_atoms, f_bonds, adj, W_i_w, out):
                 nc.tensor.transpose(turned[:, u, :], g_row_words[:, t, u, :], identity[:])
             return turned
 
-        def collect_tile(t, turned):
-            nc.vector.tensor_copy(
+        def collect_tile(copy, t, turned):
+            copy(
                 out=g_grouped_words[:, t * P * 2 : (t + 1) * P * 2].rearrange(
                     "k (c u) -> k c u", u=2
                 ),
@@ -222,17 +238,18 @@ def tile_mpnencoder_pa_kernel(tc, f_atoms, f_bonds, adj, W_i_w, out):
         )
         gate_atoms(0)
         gate_atoms(1)
-        gate_bonds(0, 6)
-        turn_weights(0)
-        turned_0 = turn_tile(0)
+        gate_bonds(0, 8)
+        turn_first_weights(0)
+        turn_first_weights(1)
         turn_weights(1)
+        turned_0 = turn_tile(0)
         turned_1 = turn_tile(1)
         for t in range(2, 6):
             gate_atoms(t)
-        collect_tile(0, turned_0)
+        collect_tile(nc.vector.tensor_copy, 0, turned_0)
         quantise_weights(0)
         quantise_tile(0)
-        collect_tile(1, turned_1)
+        collect_tile(nc.scalar.copy, 1, turned_1)
         quantise_weights(1)
         quantise_tile(1)
         turn_weights(2)
@@ -280,11 +297,11 @@ def tile_mpnencoder_pa_kernel(tc, f_atoms, f_bonds, adj, W_i_w, out):
                     collect(nc.scalar.copy, 3, turned)
                 if i == (1 if step == 2 else 0) and step + 1 < STEPS:
                     quantise_pairs(step + 1)
-                if i == 0 and step == 1:
-                    gate_bonds(6, TILES)
+                if i == 1 and step == 1:
                     gate_atoms(6)
                     gate_atoms(7)
                 if i == 0 and step == 2:
+                    gate_bonds(8, TILES)
                     gate_atoms(8)
                     gate_atoms(9)
             if step > 3:

@@ -221,7 +221,8 @@ def tile_mpnencoder_pa_kernel(tc, f_atoms, f_bonds, adj, W_i_w, out):
         zeros = keep.tile([P, P], BF16)
         nc.vector.memset(zeros[:], 0.0)
         warm = acc_psum.tile([P, 4, P], F32, tag="acc")
-        for i in range(4):
+
+        def keep_warm():
             nc.tensor.matmul(
                 warm[:],
                 lhsT=zeros[:],
@@ -229,6 +230,9 @@ def tile_mpnencoder_pa_kernel(tc, f_atoms, f_bonds, adj, W_i_w, out):
                 start=True,
                 stop=True,
             )
+
+        for i in range(4):
+            keep_warm()
         nc.vector.tensor_copy(
             out=adj_twice[:], in_=adj_cols[:].unsqueeze(2).to_broadcast([P, TILES, 2])
         )
@@ -240,10 +244,13 @@ def tile_mpnencoder_pa_kernel(tc, f_atoms, f_bonds, adj, W_i_w, out):
         gate_atoms(1)
         gate_bonds(0, 8)
         turn_first_weights(0)
+        keep_warm()
         turn_first_weights(1)
+        keep_warm()
         turn_weights(1)
         turned_0 = turn_tile(0)
         turned_1 = turn_tile(1)
+        keep_warm()
         for t in range(2, 6):
             gate_atoms(t)
         collect_tile(nc.vector.tensor_copy, 0, turned_0)

@@ -25,6 +25,7 @@ BOND_K = BOND_F // PACK
 N_PASS = 512
 W_GROUPS = 4
 W_GROUP_H = H // W_GROUPS
+FIRST_TILES = 4
 STEP_TILES = 2
 STEPS = TILES // STEP_TILES
 STEP_WORDS = STEP_TILES * P * 2
@@ -43,30 +44,29 @@ def tile_mpnencoder_pa_kernel(tc, f_atoms, f_bonds, adj, W_i_w, out):
 
     with ExitStack() as ctx:
         keep = ctx.enter_context(tc.tile_pool(name="keep", bufs=1))
-        results = ctx.enter_context(tc.tile_pool(name="results", bufs=STEPS))
+        results = ctx.enter_context(tc.tile_pool(name="results", bufs=STEPS - 2))
         turn_psum = ctx.enter_context(tc.psum_pool(name="turn_psum", bufs=2))
         acc_psum = ctx.enter_context(tc.psum_pool(name="acc_psum", bufs=6))
         ctx.enter_context(tc.manual_schedule())
 
         adj_cols = keep.tile([P, TILES], BF16)
         atoms = keep.tile([P, ATOM_F], BF16)
+        bonds_first = keep.tile([P, FIRST_TILES * BOND_F], BF16)
         bonds = keep.tile([P, TILES * BOND_F], BF16)
         w_sb = keep.tile([P, W_GROUPS, 2, F], BF16)
 
-        def load_weights(g):
-            nc.sync.dma_start(out=w_sb[:, g].rearrange("p r f -> p (r f)"), in_=w_rows[g])
-
-        def load_first_weights(r):
-            nc.sync.dma_start(out=w_sb[:, 0, r], in_=W_i_w[r * P : (r + 1) * P, :])
-
-        load_first_weights(0)
+        nc.sync.dma_start(out=w_sb[:, 0, 0], in_=W_i_w[0:P, :])
         nc.sync.dma_start(out=adj_cols[:], in_=adj_rows)
         for s in range(2):
             nc.sync.dma_start(out=atoms[s:P:2, :], in_=atom_rows)
-        load_first_weights(1)
+        nc.sync.dma_start(out=w_sb[:, 0, 1], in_=W_i_w[P : 2 * P, :])
+        nc.sync.dma_start(out=w_sb[:, 1].rearrange("p r f -> p (r f)"), in_=w_rows[1])
+        nc.sync.dma_start(out=bonds_first[:], in_=bond_rows[:, 0 : FIRST_TILES * BOND_F])
+        nc.sync.dma_start(
+            out=w_sb[:, 2:4].rearrange("p g r f -> p g (r f)"),
+            in_=W_i_w[2 * W_GROUP_H : H].rearrange("(g p r) f -> p g (r f)", p=P, r=2),
+        )
         nc.sync.dma_start(out=bonds[:], in_=bond_rows)
-        for g in range(1, W_GROUPS):
-            load_weights(g)
 
         identity = keep.tile([P, P], F32)
         make_identity(nc, identity[:])
@@ -146,25 +146,41 @@ def tile_mpnencoder_pa_kernel(tc, f_atoms, f_bonds, adj, W_i_w, out):
                 in_=g_grouped[:, step * STEP_WORDS * 2 : (step + 1) * STEP_WORDS * 2],
             )
 
-        def turn_weights(g):
+        def turn_weights(g, copy=None):
             turned = acc_psum.tile([P, 2, 2, P], F32, tag="acc")
             for r in range(2):
                 words = w_sb[:, g, r, :].bitcast(F32).rearrange("p (k u) -> p u k", u=2)
                 for u in range(2):
                     nc.tensor.transpose(turned[:, r, u, :], words[:, u, :], identity[:])
-            nc.scalar.copy(
+            (copy or nc.scalar.copy)(
                 out=w_grouped_words[:, g * W_GROUP_H * 2 : (g + 1) * W_GROUP_H * 2].rearrange(
                     "k (p w) -> k p w", w=4
                 ),
                 in_=turned[:].rearrange("k r u p -> k p (r u)"),
             )
 
-        def turn_first_weights(r):
+        def put_weights(g):
+            turned = acc_psum.tile([P, 2, 2, P], F32, tag="acc")
+            for r in range(2):
+                words = w_sb[:, g, r, :].bitcast(F32).rearrange("p (k u) -> p u k", u=2)
+                for u in range(2):
+                    nc.tensor.transpose(turned[:, r, u, :], words[:, u, :], identity[:])
+            return turned
+
+        def collect_weights(copy, g, turned):
+            copy(
+                out=w_grouped_words[:, g * W_GROUP_H * 2 : (g + 1) * W_GROUP_H * 2].rearrange(
+                    "k (p w) -> k p w", w=4
+                ),
+                in_=turned[:].rearrange("k r u p -> k p (r u)"),
+            )
+
+        def turn_first_weights(r, copy=None):
             turned = acc_psum.tile([P, 2, P], F32, tag="acc")
             words = w_sb[:, 0, r, :].bitcast(F32).rearrange("p (k u) -> p u k", u=2)
             for u in range(2):
                 nc.tensor.transpose(turned[:, u, :], words[:, u, :], identity[:])
-            nc.scalar.copy(
+            (copy or nc.scalar.copy)(
                 out=w_grouped_words[:, r * P * 2 : (r + 1) * P * 2].rearrange(
                     "k (p u) -> k p u", u=2
                 ),
@@ -183,6 +199,21 @@ def tile_mpnencoder_pa_kernel(tc, f_atoms, f_bonds, adj, W_i_w, out):
             pairs = slice(t * P, (t + 1) * P)
             h_cols = slice(half * N_PASS, (half + 1) * N_PASS)
             acc = acc_psum.tile([P, N_PASS], F32, tag="acc")
+            nc.tensor.matmul_mx(
+                out=acc[:],
+                lhsT=g_codes[:, pairs].bitcast(FP8X4),
+                lhsT_scale=g_scales[:, pairs],
+                rhs=w_codes[:, h_cols].bitcast(FP8X4),
+                rhs_scale=w_scales[:, h_cols],
+                start=True,
+                stop=True,
+            )
+            return acc
+
+        def multiply_quarter(t, quarter):
+            pairs = slice(t * P, (t + 1) * P)
+            h_cols = slice(quarter * W_GROUP_H, (quarter + 1) * W_GROUP_H)
+            acc = acc_psum.tile([P, W_GROUP_H], F32, tag="acc")
             nc.tensor.matmul_mx(
                 out=acc[:],
                 lhsT=g_codes[:, pairs].bitcast(FP8X4),
@@ -218,6 +249,56 @@ def tile_mpnencoder_pa_kernel(tc, f_atoms, f_bonds, adj, W_i_w, out):
                 in_=g_grouped[:, t * P * PACK : (t + 1) * P * PACK],
             )
 
+        g_first = keep.tile([P, FIRST_TILES, F], BF16)
+        g_first_words = (
+            g_first[:]
+            .rearrange("p t f -> p (t f)")
+            .bitcast(F32)
+            .rearrange("p (t k u) -> p t u k", t=FIRST_TILES, u=2)
+        )
+
+        def gate_first(t):
+            adj_t = adj_cols[:, t : t + 1]
+            nc.vector.tensor_scalar_mul(
+                out=g_first[:, t, 0:ATOM_F], in0=atoms[:], scalar1=adj_t
+            )
+            nc.vector.tensor_scalar_mul(
+                out=g_first[:, t, ATOM_F:ATOM_COLS], in0=atoms[:, TAIL_START:ATOM_F], scalar1=adj_t
+            )
+
+        def gate_first_bonds(t):
+            nc.vector.tensor_scalar_mul(
+                out=g_first[:, t, ATOM_COLS:F].rearrange("p (c w) -> p c w", c=2),
+                in0=bonds_first[:, t * BOND_F : (t + 1) * BOND_F]
+                .unsqueeze(1)
+                .to_broadcast([P, 2, BOND_F]),
+                scalar1=adj_cols[:, t : t + 1],
+            )
+
+        def sort_atoms():
+            nc.vector.tensor_copy(
+                out=adj_twice[:], in_=adj_cols[:].unsqueeze(2).to_broadcast([P, TILES, 2])
+            )
+            nc.vector.tensor_copy(out=atoms_sorted[:, :, 0:ATOM_K], in_=atom_words)
+            nc.vector.tensor_copy(
+                out=atoms_sorted[:, :, ATOM_K:ATOMS_K], in_=atom_words[:, :, TAIL_K:ATOM_K]
+            )
+
+        def turn_first(t):
+            turned = turn_psum.tile([P, 2, P], F32, tag="turned")
+            for u in range(2):
+                nc.tensor.transpose(turned[:, u, :], g_first_words[:, t, u, :], identity[:])
+            return turned
+
+        def turn_first_pair(t):
+            turned = acc_psum.tile([P, STEP_TILES, 2, P], F32, tag="acc")
+            for i in range(STEP_TILES):
+                for u in range(2):
+                    nc.tensor.transpose(
+                        turned[:, i, u, :], g_first_words[:, t + i, u, :], identity[:]
+                    )
+            return turned
+
         zeros = keep.tile([P, P], BF16)
         nc.vector.memset(zeros[:], 0.0)
         warm = acc_psum.tile([P, 4, P], F32, tag="acc")
@@ -231,65 +312,79 @@ def tile_mpnencoder_pa_kernel(tc, f_atoms, f_bonds, adj, W_i_w, out):
                 stop=True,
             )
 
-        for i in range(4):
-            keep_warm()
-        nc.vector.tensor_copy(
-            out=adj_twice[:], in_=adj_cols[:].unsqueeze(2).to_broadcast([P, TILES, 2])
-        )
-        nc.vector.tensor_copy(out=atoms_sorted[:, :, 0:ATOM_K], in_=atom_words)
-        nc.vector.tensor_copy(
-            out=atoms_sorted[:, :, ATOM_K:ATOMS_K], in_=atom_words[:, :, TAIL_K:ATOM_K]
-        )
-        gate_atoms(0)
-        gate_atoms(1)
-        gate_bonds(0, 8)
-        turn_first_weights(0)
-        keep_warm()
-        turn_first_weights(1)
-        keep_warm()
-        turn_weights(1)
-        turned_0 = turn_tile(0)
-        turned_1 = turn_tile(1)
-        keep_warm()
-        for t in range(2, 6):
-            gate_atoms(t)
-        collect_tile(nc.vector.tensor_copy, 0, turned_0)
-        quantise_weights(0)
-        quantise_tile(0)
-        collect_tile(nc.scalar.copy, 1, turned_1)
-        quantise_weights(1)
-        quantise_tile(1)
-        turn_weights(2)
-        turn_weights(3)
-        quantise_weights(2)
-        quantise_weights(3)
-        turned = turn(1)
-        collect(nc.vector.tensor_copy, 1, turned)
+        first = keep.tile([P, 2, STEP_TILES, H], F32, name="first")
 
-        first = results.tile([P, STEP_TILES, H], F32, name="result")
-
-        def leave(t, half, acc):
-            nc.scalar.copy(out=half_of(first[:, t], half), in_=acc[:])
+        def leave(copy, t, half, acc):
+            copy(out=half_of(first[:, t // 2, t % 2], half), in_=acc[:])
             nc.sync.dma_start(
                 out=out_rows[:, t, half * N_PASS : (half + 1) * N_PASS],
-                in_=half_of(first[:, t], half),
+                in_=half_of(first[:, t // 2, t % 2], half),
             )
 
-        acc_0 = multiply(0, 0)
-        acc_1 = multiply(1, 0)
-        turned = turn(2)
-        leave(0, 0, acc_0)
-        leave(1, 0, acc_1)
+        for i in range(4):
+            keep_warm()
+        turn_first_weights(0)
+        gate_first(0)
+        gate_first(1)
+        gate_first(2)
+        gate_first(3)
+        turn_first_weights(1)
+        turned_w1 = put_weights(1)
+        sort_atoms()
+        gate_first_bonds(0)
+        gate_first_bonds(1)
+        turned_0 = turn_first(0)
+        turned_1 = turn_first(1)
+        gate_first_bonds(2)
+        gate_first_bonds(3)
+        turned_2 = turn_first_pair(2)
+        gate_atoms(4)
+        gate_atoms(5)
+        collect_weights(nc.scalar.copy, 1, turned_w1)
+        quantise_weights(0)
+        collect_tile(nc.vector.tensor_copy, 0, turned_0)
+        collect_tile(nc.scalar.copy, 1, turned_1)
+        quantise_tile(0)
+        collect(nc.scalar.copy, 1, turned_2)
+        quantise_weights(1)
+        turned_w2 = put_weights(2)
+        turned_w3 = put_weights(3)
+        quantise_tile(1)
+        acc_0_0 = multiply(0, 0)
+        acc_1_0 = multiply(1, 0)
+        collect_weights(nc.scalar.copy, 2, turned_w2)
+        gate_bonds(4, 8)
         quantise_pairs(1)
+        acc_2_0 = multiply(2, 0)
+        acc_3_0 = multiply(3, 0)
+        leave(nc.vector.tensor_copy, 0, 0, acc_0_0)
+        collect_weights(nc.scalar.copy, 3, turned_w3)
+        leave(nc.scalar.copy, 1, 0, acc_1_0)
+        quantise_weights(2)
+        quantise_weights(3)
+        turned = turn(2)
+        leave(nc.scalar.copy, 2, 0, acc_2_0)
+        leave(nc.vector.tensor_copy, 3, 0, acc_3_0)
+        acc_0_1 = multiply(0, 1)
+        acc_1_1 = multiply(1, 1)
         collect(nc.vector.tensor_copy, 2, turned)
-        acc_0 = multiply(0, 1)
-        acc_1 = multiply(1, 1)
-        leave(0, 1, acc_0)
-        leave(1, 1, acc_1)
+        acc_2_1 = multiply(2, 1)
+        acc_3_1 = multiply(3, 1)
+        leave(nc.scalar.copy, 0, 1, acc_0_1)
+        gate_atoms(6)
+        gate_atoms(7)
+        turned = turn(3)
+        leave(nc.scalar.copy, 1, 1, acc_1_1)
+        quantise_pairs(2)
+        leave(nc.vector.tensor_copy, 2, 1, acc_2_1)
+        gate_bonds(8, 16)
+        gate_atoms(8)
+        gate_atoms(9)
+        leave(nc.scalar.copy, 3, 1, acc_3_1)
 
-        for step in range(1, STEPS):
+        for step in range(2, STEPS):
             result = results.tile([P, STEP_TILES, H], F32, name="result")
-            if step > 2 and step + 1 < STEPS:
+            if step + 1 < STEPS:
                 collect(nc.scalar.copy, step + 1, turned)
             for i in range(STEP_TILES):
                 t = step * STEP_TILES + i
@@ -299,24 +394,14 @@ def tile_mpnencoder_pa_kernel(tc, f_atoms, f_bonds, adj, W_i_w, out):
                 nc.scalar.copy(out=half_of(result[:, i], 1), in_=acc[:])
                 if step <= 3:
                     nc.sync.dma_start(out=out_rows[:, t, :], in_=result[:, i])
-                if step == 2 and i == 0:
-                    turned = turn(3)
-                    collect(nc.scalar.copy, 3, turned)
-                if i == (1 if step == 2 else 0) and step + 1 < STEPS:
+                if i == 0 and step + 1 < STEPS:
                     quantise_pairs(step + 1)
-                if i == 1 and step == 1:
-                    gate_atoms(6)
-                    gate_atoms(7)
-                if i == 0 and step == 2:
-                    gate_bonds(8, TILES)
-                    gate_atoms(8)
-                    gate_atoms(9)
             if step > 3:
                 nc.sync.dma_start(
                     out=out_rows[:, step * STEP_TILES : (step + 1) * STEP_TILES, :], in_=result[:]
                 )
-            if step > 1 and step + 2 < STEPS:
+            if step + 2 < STEPS:
                 turned = turn(step + 2)
-            if step > 1 and step + 3 < STEPS:
+            if step + 3 < STEPS:
                 gate_atoms((step + 3) * STEP_TILES)
                 gate_atoms((step + 3) * STEP_TILES + 1)

@@ -25,7 +25,8 @@ BOND_K = BOND_F // PACK
 N_PASS = 512
 W_GROUPS = 4
 W_GROUP_H = H // W_GROUPS
-FIRST_TILES = 4
+FIRST_TILES = 2
+FIRST_BONDS = 8
 STEP_TILES = 2
 STEPS = TILES // STEP_TILES
 STEP_WORDS = STEP_TILES * P * 2
@@ -45,13 +46,11 @@ def tile_mpnencoder_pa_kernel(tc, f_atoms, f_bonds, adj, W_i_w, out):
     with ExitStack() as ctx:
         keep = ctx.enter_context(tc.tile_pool(name="keep", bufs=1))
         results = ctx.enter_context(tc.tile_pool(name="results", bufs=STEPS - 2))
-        turn_psum = ctx.enter_context(tc.psum_pool(name="turn_psum", bufs=2))
-        acc_psum = ctx.enter_context(tc.psum_pool(name="acc_psum", bufs=6))
+        psum = ctx.enter_context(tc.psum_pool(name="psum", bufs=8))
         ctx.enter_context(tc.manual_schedule())
 
         adj_cols = keep.tile([P, TILES], BF16)
         atoms = keep.tile([P, ATOM_F], BF16)
-        bonds_first = keep.tile([P, FIRST_TILES * BOND_F], BF16)
         bonds = keep.tile([P, TILES * BOND_F], BF16)
         w_sb = keep.tile([P, W_GROUPS, 2, F], BF16)
 
@@ -59,14 +58,12 @@ def tile_mpnencoder_pa_kernel(tc, f_atoms, f_bonds, adj, W_i_w, out):
         nc.sync.dma_start(out=adj_cols[:], in_=adj_rows)
         for s in range(2):
             nc.sync.dma_start(out=atoms[s:P:2, :], in_=atom_rows)
+        nc.sync.dma_start(out=bonds[:, 0 : FIRST_BONDS * BOND_F], in_=bond_rows[:, 0 : FIRST_BONDS * BOND_F])
         nc.sync.dma_start(out=w_sb[:, 0, 1], in_=W_i_w[P : 2 * P, :])
         nc.sync.dma_start(out=w_sb[:, 1].rearrange("p r f -> p (r f)"), in_=w_rows[1])
-        nc.sync.dma_start(out=bonds_first[:], in_=bond_rows[:, 0 : FIRST_TILES * BOND_F])
-        nc.sync.dma_start(
-            out=w_sb[:, 2:4].rearrange("p g r f -> p g (r f)"),
-            in_=W_i_w[2 * W_GROUP_H : H].rearrange("(g p r) f -> p g (r f)", p=P, r=2),
-        )
-        nc.sync.dma_start(out=bonds[:], in_=bond_rows)
+        nc.sync.dma_start(out=w_sb[:, 2].rearrange("p r f -> p (r f)"), in_=w_rows[2])
+        nc.sync.dma_start(out=w_sb[:, 3].rearrange("p r f -> p (r f)"), in_=w_rows[3])
+        nc.sync.dma_start(out=bonds[:, FIRST_BONDS * BOND_F :], in_=bond_rows[:, FIRST_BONDS * BOND_F :])
 
         identity = keep.tile([P, P], F32)
         make_identity(nc, identity[:])
@@ -122,7 +119,7 @@ def tile_mpnencoder_pa_kernel(tc, f_atoms, f_bonds, adj, W_i_w, out):
                     )
 
         def turn(step):
-            turned = turn_psum.tile([P, STEP_TILES, 2, P], F32, tag="turned")
+            turned = psum.tile([P, STEP_TILES, 2, P], F32, tag="bank")
             for i in range(STEP_TILES):
                 for u in range(2):
                     nc.tensor.transpose(
@@ -147,7 +144,7 @@ def tile_mpnencoder_pa_kernel(tc, f_atoms, f_bonds, adj, W_i_w, out):
             )
 
         def turn_weights(g, copy=None):
-            turned = acc_psum.tile([P, 2, 2, P], F32, tag="acc")
+            turned = psum.tile([P, 2, 2, P], F32, tag="bank")
             for r in range(2):
                 words = w_sb[:, g, r, :].bitcast(F32).rearrange("p (k u) -> p u k", u=2)
                 for u in range(2):
@@ -159,8 +156,23 @@ def tile_mpnencoder_pa_kernel(tc, f_atoms, f_bonds, adj, W_i_w, out):
                 in_=turned[:].rearrange("k r u p -> k p (r u)"),
             )
 
+        def put_half_weights(g, r):
+            turned = psum.tile([P, 2, P], F32, tag="bank")
+            words = w_sb[:, g, r, :].bitcast(F32).rearrange("p (k u) -> p u k", u=2)
+            for u in range(2):
+                nc.tensor.transpose(turned[:, u, :], words[:, u, :], identity[:])
+            return turned
+
+        def collect_half_weights(copy, g, r, turned):
+            copy(
+                out=w_grouped_words[:, g * W_GROUP_H * 2 : (g + 1) * W_GROUP_H * 2].rearrange(
+                    "k (p r u) -> k p r u", r=2, u=2
+                )[:, :, r],
+                in_=turned[:].rearrange("k u p -> k p u"),
+            )
+
         def put_weights(g):
-            turned = acc_psum.tile([P, 2, 2, P], F32, tag="acc")
+            turned = psum.tile([P, 2, 2, P], F32, tag="bank")
             for r in range(2):
                 words = w_sb[:, g, r, :].bitcast(F32).rearrange("p (k u) -> p u k", u=2)
                 for u in range(2):
@@ -176,7 +188,7 @@ def tile_mpnencoder_pa_kernel(tc, f_atoms, f_bonds, adj, W_i_w, out):
             )
 
         def turn_first_weights(r, copy=None):
-            turned = acc_psum.tile([P, 2, P], F32, tag="acc")
+            turned = psum.tile([P, 2, P], F32, tag="bank")
             words = w_sb[:, 0, r, :].bitcast(F32).rearrange("p (k u) -> p u k", u=2)
             for u in range(2):
                 nc.tensor.transpose(turned[:, u, :], words[:, u, :], identity[:])
@@ -198,7 +210,7 @@ def tile_mpnencoder_pa_kernel(tc, f_atoms, f_bonds, adj, W_i_w, out):
         def multiply(t, half):
             pairs = slice(t * P, (t + 1) * P)
             h_cols = slice(half * N_PASS, (half + 1) * N_PASS)
-            acc = acc_psum.tile([P, N_PASS], F32, tag="acc")
+            acc = psum.tile([P, N_PASS], F32, tag="bank")
             nc.tensor.matmul_mx(
                 out=acc[:],
                 lhsT=g_codes[:, pairs].bitcast(FP8X4),
@@ -213,7 +225,7 @@ def tile_mpnencoder_pa_kernel(tc, f_atoms, f_bonds, adj, W_i_w, out):
         def multiply_quarter(t, quarter):
             pairs = slice(t * P, (t + 1) * P)
             h_cols = slice(quarter * W_GROUP_H, (quarter + 1) * W_GROUP_H)
-            acc = acc_psum.tile([P, W_GROUP_H], F32, tag="acc")
+            acc = psum.tile([P, W_GROUP_H], F32, tag="bank")
             nc.tensor.matmul_mx(
                 out=acc[:],
                 lhsT=g_codes[:, pairs].bitcast(FP8X4),
@@ -229,7 +241,7 @@ def tile_mpnencoder_pa_kernel(tc, f_atoms, f_bonds, adj, W_i_w, out):
             return result[:, half * N_PASS : (half + 1) * N_PASS]
 
         def turn_tile(t):
-            turned = turn_psum.tile([P, 2, P], F32, tag="turned")
+            turned = psum.tile([P, 2, P], F32, tag="bank")
             for u in range(2):
                 nc.tensor.transpose(turned[:, u, :], g_row_words[:, t, u, :], identity[:])
             return turned
@@ -269,39 +281,32 @@ def tile_mpnencoder_pa_kernel(tc, f_atoms, f_bonds, adj, W_i_w, out):
         def gate_first_bonds(t):
             nc.vector.tensor_scalar_mul(
                 out=g_first[:, t, ATOM_COLS:F].rearrange("p (c w) -> p c w", c=2),
-                in0=bonds_first[:, t * BOND_F : (t + 1) * BOND_F]
+                in0=bonds[:, t * BOND_F : (t + 1) * BOND_F]
                 .unsqueeze(1)
                 .to_broadcast([P, 2, BOND_F]),
                 scalar1=adj_cols[:, t : t + 1],
             )
 
-        def sort_atoms():
+        def spread_adj():
             nc.vector.tensor_copy(
                 out=adj_twice[:], in_=adj_cols[:].unsqueeze(2).to_broadcast([P, TILES, 2])
             )
+
+        def sort_atoms():
             nc.vector.tensor_copy(out=atoms_sorted[:, :, 0:ATOM_K], in_=atom_words)
             nc.vector.tensor_copy(
                 out=atoms_sorted[:, :, ATOM_K:ATOMS_K], in_=atom_words[:, :, TAIL_K:ATOM_K]
             )
 
         def turn_first(t):
-            turned = turn_psum.tile([P, 2, P], F32, tag="turned")
+            turned = psum.tile([P, 2, P], F32, tag="bank")
             for u in range(2):
                 nc.tensor.transpose(turned[:, u, :], g_first_words[:, t, u, :], identity[:])
             return turned
 
-        def turn_first_pair(t):
-            turned = acc_psum.tile([P, STEP_TILES, 2, P], F32, tag="acc")
-            for i in range(STEP_TILES):
-                for u in range(2):
-                    nc.tensor.transpose(
-                        turned[:, i, u, :], g_first_words[:, t + i, u, :], identity[:]
-                    )
-            return turned
-
         zeros = keep.tile([P, P], BF16)
         nc.vector.memset(zeros[:], 0.0)
-        warm = acc_psum.tile([P, 4, P], F32, tag="acc")
+        warm = psum.tile([P, 4, P], F32, tag="bank")
 
         def keep_warm():
             nc.tensor.matmul(
@@ -321,66 +326,88 @@ def tile_mpnencoder_pa_kernel(tc, f_atoms, f_bonds, adj, W_i_w, out):
                 in_=half_of(first[:, t // 2, t % 2], half),
             )
 
+        def leave_quarter(copy, t, quarter, acc):
+            h_cols = slice(quarter * W_GROUP_H, (quarter + 1) * W_GROUP_H)
+            copy(out=first[:, t // 2, t % 2, h_cols], in_=acc[:])
+
+        def store_quarters(t, quarter):
+            h_cols = slice(quarter * W_GROUP_H, (quarter + 1) * W_GROUP_H)
+            nc.sync.dma_start(out=out_rows[:, t : t + 2, h_cols], in_=first[:, t // 2, :, h_cols])
+
+        def store_quarter(t, quarter):
+            h_cols = slice(quarter * W_GROUP_H, (quarter + 1) * W_GROUP_H)
+            nc.sync.dma_start(out=out_rows[:, t, h_cols], in_=first[:, t // 2, t % 2, h_cols])
+
         for i in range(4):
             keep_warm()
         turn_first_weights(0)
         gate_first(0)
-        gate_first(1)
-        gate_first(2)
-        gate_first(3)
-        turn_first_weights(1)
-        turned_w1 = put_weights(1)
-        sort_atoms()
         gate_first_bonds(0)
+        gate_first(1)
         gate_first_bonds(1)
+        keep_warm()
         turned_0 = turn_first(0)
+        collect_tile(nc.scalar.copy, 0, turned_0)
+        turn_first_weights(1)
         turned_1 = turn_first(1)
-        gate_first_bonds(2)
-        gate_first_bonds(3)
-        turned_2 = turn_first_pair(2)
+        keep_warm()
+        spread_adj()
+        sort_atoms()
+        gate_atoms(2)
+        gate_atoms(3)
+        gate_bonds(2, 8)
+        collect_tile(nc.scalar.copy, 1, turned_1)
+        turned_w1 = put_weights(1)
+        turned_p1 = turn(1)
+        quantise_tile(0)
+        quantise_weights(0)
+        quantise_tile(1)
         gate_atoms(4)
         gate_atoms(5)
         collect_weights(nc.scalar.copy, 1, turned_w1)
-        quantise_weights(0)
-        collect_tile(nc.vector.tensor_copy, 0, turned_0)
-        collect_tile(nc.scalar.copy, 1, turned_1)
-        quantise_tile(0)
-        collect(nc.scalar.copy, 1, turned_2)
-        quantise_weights(1)
         turned_w2 = put_weights(2)
-        turned_w3 = put_weights(3)
-        quantise_tile(1)
-        acc_0_0 = multiply(0, 0)
-        acc_1_0 = multiply(1, 0)
+        keep_warm()
+        acc_q0_0 = multiply_quarter(0, 0)
+        acc_q1_0 = multiply_quarter(1, 0)
+        collect(nc.vector.tensor_copy, 1, turned_p1)
+        quantise_weights(1)
         collect_weights(nc.scalar.copy, 2, turned_w2)
-        gate_bonds(4, 8)
+        turned_w3 = put_weights(3)
+        leave_quarter(nc.vector.tensor_copy, 0, 0, acc_q0_0)
+        store_quarter(0, 0)
+        leave_quarter(nc.scalar.copy, 1, 0, acc_q1_0)
+        store_quarter(1, 0)
         quantise_pairs(1)
+        acc_q0_1 = multiply_quarter(0, 1)
+        acc_q1_1 = multiply_quarter(1, 1)
         acc_2_0 = multiply(2, 0)
         acc_3_0 = multiply(3, 0)
-        leave(nc.vector.tensor_copy, 0, 0, acc_0_0)
-        collect_weights(nc.scalar.copy, 3, turned_w3)
-        leave(nc.scalar.copy, 1, 0, acc_1_0)
-        quantise_weights(2)
-        quantise_weights(3)
         turned = turn(2)
+        quantise_weights(2)
+        collect_weights(nc.scalar.copy, 3, turned_w3)
+        leave_quarter(nc.vector.tensor_copy, 0, 1, acc_q0_1)
+        store_quarter(0, 1)
+        leave_quarter(nc.scalar.copy, 1, 1, acc_q1_1)
+        store_quarter(1, 1)
         leave(nc.scalar.copy, 2, 0, acc_2_0)
+        quantise_weights(3)
         leave(nc.vector.tensor_copy, 3, 0, acc_3_0)
+        collect(nc.scalar.copy, 2, turned)
         acc_0_1 = multiply(0, 1)
         acc_1_1 = multiply(1, 1)
-        collect(nc.vector.tensor_copy, 2, turned)
         acc_2_1 = multiply(2, 1)
         acc_3_1 = multiply(3, 1)
-        leave(nc.scalar.copy, 0, 1, acc_0_1)
         gate_atoms(6)
         gate_atoms(7)
-        turned = turn(3)
+        leave(nc.vector.tensor_copy, 0, 1, acc_0_1)
         leave(nc.scalar.copy, 1, 1, acc_1_1)
         quantise_pairs(2)
+        turned = turn(3)
         leave(nc.vector.tensor_copy, 2, 1, acc_2_1)
+        leave(nc.scalar.copy, 3, 1, acc_3_1)
         gate_bonds(8, 16)
         gate_atoms(8)
         gate_atoms(9)
-        leave(nc.scalar.copy, 3, 1, acc_3_1)
 
         for step in range(2, STEPS):
             result = results.tile([P, STEP_TILES, H], F32, name="result")

@@ -45,7 +45,8 @@ def tile_mpnencoder_pa_kernel(tc, f_atoms, f_bonds, adj, W_i_w, out):
 
     with ExitStack() as ctx:
         keep = ctx.enter_context(tc.tile_pool(name="keep", bufs=1))
-        results = ctx.enter_context(tc.tile_pool(name="results", bufs=STEPS - 2))
+        results = ctx.enter_context(tc.tile_pool(name="results", bufs=STEPS - 3))
+        wide_results = ctx.enter_context(tc.tile_pool(name="wide_results", bufs=1))
         psum = ctx.enter_context(tc.psum_pool(name="psum", bufs=8))
         ctx.enter_context(tc.manual_schedule())
 
@@ -341,6 +342,7 @@ def tile_mpnencoder_pa_kernel(tc, f_atoms, f_bonds, adj, W_i_w, out):
         for i in range(4):
             keep_warm()
         turn_first_weights(0)
+        spread_adj()
         gate_first(0)
         gate_first_bonds(0)
         gate_first(1)
@@ -351,11 +353,10 @@ def tile_mpnencoder_pa_kernel(tc, f_atoms, f_bonds, adj, W_i_w, out):
         turn_first_weights(1)
         turned_1 = turn_first(1)
         keep_warm()
-        spread_adj()
         sort_atoms()
+        gate_bonds(2, 8)
         gate_atoms(2)
         gate_atoms(3)
-        gate_bonds(2, 8)
         collect_tile(nc.scalar.copy, 1, turned_1)
         turned_w1 = put_weights(1)
         turned_p1 = turn(1)
@@ -419,11 +420,11 @@ def tile_mpnencoder_pa_kernel(tc, f_atoms, f_bonds, adj, W_i_w, out):
                 nc.vector.tensor_copy(out=half_of(result[:, i], 0), in_=acc[:])
                 acc = multiply(t, 1)
                 nc.scalar.copy(out=half_of(result[:, i], 1), in_=acc[:])
-                if step <= 3:
+                if step <= 2:
                     nc.sync.dma_start(out=out_rows[:, t, :], in_=result[:, i])
                 if i == 0 and step + 1 < STEPS:
                     quantise_pairs(step + 1)
-            if step > 3:
+            if step > 2:
                 nc.sync.dma_start(
                     out=out_rows[:, step * STEP_TILES : (step + 1) * STEP_TILES, :], in_=result[:]
                 )

@@ -45,8 +45,7 @@ def tile_mpnencoder_pa_kernel(tc, f_atoms, f_bonds, adj, W_i_w, out):
 
     with ExitStack() as ctx:
         keep = ctx.enter_context(tc.tile_pool(name="keep", bufs=1))
-        results = ctx.enter_context(tc.tile_pool(name="results", bufs=STEPS - 3))
-        wide_results = ctx.enter_context(tc.tile_pool(name="wide_results", bufs=1))
+        results = ctx.enter_context(tc.tile_pool(name="results", bufs=STEPS - 2))
         psum = ctx.enter_context(tc.psum_pool(name="psum", bufs=8))
         ctx.enter_context(tc.manual_schedule())
 
@@ -67,6 +66,8 @@ def tile_mpnencoder_pa_kernel(tc, f_atoms, f_bonds, adj, W_i_w, out):
         nc.sync.dma_start(out=bonds[:, FIRST_BONDS * BOND_F :], in_=bond_rows[:, FIRST_BONDS * BOND_F :])
 
         identity = keep.tile([P, P], F32)
+        zeros = keep.tile([P, P], BF16)
+        nc.gpsimd.memset(zeros[:], 0.0)
         make_identity(nc, identity[:])
 
         atoms_sorted = keep.tile([P, 2, ATOMS_K], F32)
@@ -305,8 +306,6 @@ def tile_mpnencoder_pa_kernel(tc, f_atoms, f_bonds, adj, W_i_w, out):
                 nc.tensor.transpose(turned[:, u, :], g_first_words[:, t, u, :], identity[:])
             return turned
 
-        zeros = keep.tile([P, P], BF16)
-        nc.vector.memset(zeros[:], 0.0)
         warm = psum.tile([P, 4, P], F32, tag="bank")
 
         def keep_warm():
@@ -341,71 +340,70 @@ def tile_mpnencoder_pa_kernel(tc, f_atoms, f_bonds, adj, W_i_w, out):
 
         for i in range(4):
             keep_warm()
-        turn_first_weights(0)
         spread_adj()
+        turn_first_weights(0)
         gate_first(0)
         gate_first_bonds(0)
         gate_first(1)
         gate_first_bonds(1)
         keep_warm()
-        turned_0 = turn_first(0)
-        collect_tile(nc.scalar.copy, 0, turned_0)
         turn_first_weights(1)
+        turned_0 = turn_first(0)
         turned_1 = turn_first(1)
-        keep_warm()
         sort_atoms()
         gate_bonds(2, 8)
         gate_atoms(2)
         gate_atoms(3)
+        collect_tile(nc.vector.tensor_copy, 0, turned_0)
         collect_tile(nc.scalar.copy, 1, turned_1)
         turned_w1 = put_weights(1)
-        turned_p1 = turn(1)
-        quantise_tile(0)
-        quantise_weights(0)
-        quantise_tile(1)
-        gate_atoms(4)
-        gate_atoms(5)
-        collect_weights(nc.scalar.copy, 1, turned_w1)
-        turned_w2 = put_weights(2)
         keep_warm()
+        turned_p1 = turn(1)
+        collect_weights(nc.scalar.copy, 1, turned_w1)
+        quantise_weights(0)
+        quantise_tile(0)
+        quantise_tile(1)
+        collect(nc.scalar.copy, 1, turned_p1)
+        turned_w2 = put_weights(2)
         acc_q0_0 = multiply_quarter(0, 0)
         acc_q1_0 = multiply_quarter(1, 0)
-        collect(nc.vector.tensor_copy, 1, turned_p1)
-        quantise_weights(1)
-        collect_weights(nc.scalar.copy, 2, turned_w2)
         turned_w3 = put_weights(3)
-        leave_quarter(nc.vector.tensor_copy, 0, 0, acc_q0_0)
+        leave_quarter(nc.scalar.copy, 0, 0, acc_q0_0)
         store_quarter(0, 0)
         leave_quarter(nc.scalar.copy, 1, 0, acc_q1_0)
         store_quarter(1, 0)
+        gate_atoms(4)
+        gate_atoms(5)
+        quantise_weights(1)
         quantise_pairs(1)
+        collect_weights(nc.vector.tensor_copy, 2, turned_w2)
+        collect_weights(nc.scalar.copy, 3, turned_w3)
         acc_q0_1 = multiply_quarter(0, 1)
         acc_q1_1 = multiply_quarter(1, 1)
         acc_2_0 = multiply(2, 0)
         acc_3_0 = multiply(3, 0)
         turned = turn(2)
-        quantise_weights(2)
-        collect_weights(nc.scalar.copy, 3, turned_w3)
         leave_quarter(nc.vector.tensor_copy, 0, 1, acc_q0_1)
         store_quarter(0, 1)
         leave_quarter(nc.scalar.copy, 1, 1, acc_q1_1)
         store_quarter(1, 1)
-        leave(nc.scalar.copy, 2, 0, acc_2_0)
+        quantise_weights(2)
         quantise_weights(3)
+        leave(nc.scalar.copy, 2, 0, acc_2_0)
         leave(nc.vector.tensor_copy, 3, 0, acc_3_0)
-        collect(nc.scalar.copy, 2, turned)
         acc_0_1 = multiply(0, 1)
         acc_1_1 = multiply(1, 1)
-        acc_2_1 = multiply(2, 1)
-        acc_3_1 = multiply(3, 1)
+        collect(nc.scalar.copy, 2, turned)
         gate_atoms(6)
         gate_atoms(7)
-        leave(nc.vector.tensor_copy, 0, 1, acc_0_1)
-        leave(nc.scalar.copy, 1, 1, acc_1_1)
+        acc_2_1 = multiply(2, 1)
+        acc_3_1 = multiply(3, 1)
         quantise_pairs(2)
+        leave(nc.scalar.copy, 0, 1, acc_0_1)
+        leave(nc.vector.tensor_copy, 1, 1, acc_1_1)
         turned = turn(3)
-        leave(nc.vector.tensor_copy, 2, 1, acc_2_1)
-        leave(nc.scalar.copy, 3, 1, acc_3_1)
+        leave(nc.scalar.copy, 2, 1, acc_2_1)
+        leave(nc.vector.tensor_copy, 3, 1, acc_3_1)
         gate_bonds(8, 16)
         gate_atoms(8)
         gate_atoms(9)

from contextlib import ExitStack

import concourse.mybir as mybir
from concourse.masks import make_identity

F32 = mybir.dt.float32
BF16 = mybir.dt.bfloat16
U32 = mybir.dt.uint32
U8 = mybir.dt.uint8
FP8X4 = mybir.dt.float8_e4m3fn_x4

P = 128
PACK = 4
TILES = 16
ATOM_F = 352
TAIL_START = 256
ATOM_COLS = ATOM_F + (ATOM_F - TAIL_START)
BOND_F = 32
F = ATOM_COLS + 2 * BOND_F
H = 1024
ATOM_K = ATOM_F // PACK
TAIL_K = TAIL_START // PACK
ATOMS_K = ATOM_COLS // PACK
BOND_K = BOND_F // PACK
N_PASS = 512
W_GROUPS = 4
W_GROUP_H = H // W_GROUPS
FIRST_TILES = 2
FIRST_BONDS = 8
STEP_TILES = 2
STEPS = TILES // STEP_TILES
STEP_WORDS = STEP_TILES * P * 2

FLOPS = 2 * P * TILES * F * H


def tile_mpnencoder_pa_kernel(tc, f_atoms, f_bonds, adj, W_i_w, out):
    nc = tc.nc

    atom_rows = f_atoms.rearrange("b m f -> (b m) f")
    bond_rows = f_bonds.rearrange("b m (s t) c -> (b m s) (t c)", s=2)
    adj_rows = adj.rearrange("b m (s t) -> (b m s) t", s=2)
    out_rows = out.rearrange("b m (s t) h -> (b m s) t h", s=2)
    w_rows = W_i_w.rearrange("(g p r) f -> g p (r f)", p=P, r=2)

    with ExitStack() as ctx:
        keep = ctx.enter_context(tc.tile_pool(name="keep", bufs=1))
        results = ctx.enter_context(tc.tile_pool(name="results", bufs=STEPS - 2))
        psum = ctx.enter_context(tc.psum_pool(name="psum", bufs=8))
        ctx.enter_context(tc.manual_schedule())

        adj_cols = keep.tile([P, TILES], BF16)
        atoms = keep.tile([P, ATOM_F], BF16)
        bonds = keep.tile([P, TILES * BOND_F], BF16)
        w_sb = keep.tile([P, W_GROUPS, 2, F], BF16)

        nc.sync.dma_start(out=w_sb[:, 0, 0], in_=W_i_w[0:P, :])
        nc.sync.dma_start(out=adj_cols[:], in_=adj_rows)
        for s in range(2):
            nc.sync.dma_start(out=atoms[s:P:2, :], in_=atom_rows)
        nc.sync.dma_start(out=bonds[:, 0 : FIRST_BONDS * BOND_F], in_=bond_rows[:, 0 : FIRST_BONDS * BOND_F])
        nc.sync.dma_start(out=w_sb[:, 0, 1], in_=W_i_w[P : 2 * P, :])
        nc.sync.dma_start(out=w_sb[:, 1].rearrange("p r f -> p (r f)"), in_=w_rows[1])
        nc.sync.dma_start(out=w_sb[:, 2].rearrange("p r f -> p (r f)"), in_=w_rows[2])
        nc.sync.dma_start(out=w_sb[:, 3].rearrange("p r f -> p (r f)"), in_=w_rows[3])
        nc.sync.dma_start(out=bonds[:, FIRST_BONDS * BOND_F :], in_=bond_rows[:, FIRST_BONDS * BOND_F :])

        identity = keep.tile([P, P], F32)
        zeros = keep.tile([P, P], BF16)
        nc.gpsimd.memset(zeros[:], 0.0)
        make_identity(nc, identity[:])

        atoms_sorted = keep.tile([P, 2, ATOMS_K], F32)
        adj_twice = keep.tile([P, TILES, 2], BF16)
        g_rows = keep.tile([P, TILES, 2, P * 2], BF16)
        g_grouped = keep.tile([P, TILES * P * PACK], BF16, align_bytes=64)
        g_codes = keep.tile([P, TILES * P], U32, align_bytes=64)
        g_scales = keep.tile([P, TILES * P], U8, align_bytes=64)
        w_grouped = keep.tile([P, H * PACK], BF16, align_bytes=64)
        w_codes = keep.tile([P, H], U32, align_bytes=64)
        w_scales = keep.tile([P, H], U8, align_bytes=64)

        atom_words = atoms[:].bitcast(F32).rearrange("p (k u) -> p u k", u=2)
        atoms_by_u = (
            atoms_sorted[:]
            .rearrange("p u k -> p (u k)")
            .bitcast(BF16)
            .rearrange("p (u w) -> p u w", u=2)
        )
        bonds_by_u = bonds[:].rearrange("p (t k u e) -> p t u k e", t=TILES, u=2, e=2)
        g_row_words = (
            g_rows[:]
            .rearrange("p t u w -> p (t u w)")
            .bitcast(F32)
            .rearrange("p (t u k) -> p t u k", t=TILES, u=2)
        )
        g_grouped_words = g_grouped[:].bitcast(F32)
        w_grouped_words = w_grouped[:].bitcast(F32)

        def gate_atoms(t):
            nc.vector.tensor_scalar_mul(
                out=g_rows[:, t, :, 0 : ATOMS_K * 2],
                in0=atoms_by_u,
                scalar1=adj_cols[:, t : t + 1],
            )

        def gate_bonds(first, last):
            tiles = slice(first, last)
            for u in range(2):
                for c in range(2):
                    start = (ATOMS_K + c * BOND_K) * 2
                    nc.vector.tensor_tensor(
                        out=g_rows[:, tiles, u, start : start + BOND_K * 2].rearrange(
                            "p t (k e) -> p t k e", e=2
                        ),
                        in0=bonds_by_u[:, tiles, u],
                        in1=adj_twice[:, tiles]
                        .unsqueeze(2)
                        .to_broadcast([P, last - first, BOND_K, 2]),
                        op=mybir.AluOpType.mult,
                    )

        def turn(step):
            turned = psum.tile([P, STEP_TILES, 2, P], F32, tag="bank")
            for i in range(STEP_TILES):
                for u in range(2):
                    nc.tensor.transpose(
                        turned[:, i, u, :], g_row_words[:, step * STEP_TILES + i, u, :], identity[:]
                    )
            return turned

        def collect(copy, step, turned):
            copy(
                out=g_grouped_words[:, step * STEP_WORDS : (step + 1) * STEP_WORDS].rearrange(
                    "k (i c u) -> k i c u", i=STEP_TILES, u=2
                ),
                in_=turned[:].rearrange("k i u c -> k i c u"),
            )

        def quantise_pairs(step):
            columns = slice(step * STEP_TILES * P, (step + 1) * STEP_TILES * P)
            nc.vector.quantize_mx(
                out=g_codes[:, columns].bitcast(FP8X4),
                scales=g_scales[:, columns],
                in_=g_grouped[:, step * STEP_WORDS * 2 : (step + 1) * STEP_WORDS * 2],
            )

        def turn_weights(g, copy=None):
            turned = psum.tile([P, 2, 2, P], F32, tag="bank")
            for r in range(2):
                words = w_sb[:, g, r, :].bitcast(F32).rearrange("p (k u) -> p u k", u=2)
                for u in range(2):
                    nc.tensor.transpose(turned[:, r, u, :], words[:, u, :], identity[:])
            (copy or nc.scalar.copy)(
                out=w_grouped_words[:, g * W_GROUP_H * 2 : (g + 1) * W_GROUP_H * 2].rearrange(
                    "k (p w) -> k p w", w=4
                ),
                in_=turned[:].rearrange("k r u p -> k p (r u)"),
            )

        def put_half_weights(g, r):
            turned = psum.tile([P, 2, P], F32, tag="bank")
            words = w_sb[:, g, r, :].bitcast(F32).rearrange("p (k u) -> p u k", u=2)
            for u in range(2):
                nc.tensor.transpose(turned[:, u, :], words[:, u, :], identity[:])
            return turned

        def collect_half_weights(copy, g, r, turned):
            copy(
                out=w_grouped_words[:, g * W_GROUP_H * 2 : (g + 1) * W_GROUP_H * 2].rearrange(
                    "k (p r u) -> k p r u", r=2, u=2
                )[:, :, r],
                in_=turned[:].rearrange("k u p -> k p u"),
            )

        def put_weights(g):
            turned = psum.tile([P, 2, 2, P], F32, tag="bank")
            for r in range(2):
                words = w_sb[:, g, r, :].bitcast(F32).rearrange("p (k u) -> p u k", u=2)
                for u in range(2):
                    nc.tensor.transpose(turned[:, r, u, :], words[:, u, :], identity[:])
            return turned

        def collect_weights(copy, g, turned):
            copy(
                out=w_grouped_words[:, g * W_GROUP_H * 2 : (g + 1) * W_GROUP_H * 2].rearrange(
                    "k (p w) -> k p w", w=4
                ),
                in_=turned[:].rearrange("k r u p -> k p (r u)"),
            )

        def turn_first_weights(r, copy=None):
            turned = psum.tile([P, 2, P], F32, tag="bank")
            words = w_sb[:, 0, r, :].bitcast(F32).rearrange("p (k u) -> p u k", u=2)
            for u in range(2):
                nc.tensor.transpose(turned[:, u, :], words[:, u, :], identity[:])
            (copy or nc.scalar.copy)(
                out=w_grouped_words[:, r * P * 2 : (r + 1) * P * 2].rearrange(
                    "k (p u) -> k p u", u=2
                ),
                in_=turned[:].rearrange("k u p -> k p u"),
            )

        def quantise_weights(g):
            h_rows = slice(g * W_GROUP_H, (g + 1) * W_GROUP_H)
            nc.vector.quantize_mx(
                out=w_codes[:, h_rows].bitcast(FP8X4),
                scales=w_scales[:, h_rows],
                in_=w_grouped[:, g * W_GROUP_H * PACK : (g + 1) * W_GROUP_H * PACK],
            )

        def multiply(t, half):
            pairs = slice(t * P, (t + 1) * P)
            h_cols = slice(half * N_PASS, (half + 1) * N_PASS)
            acc = psum.tile([P, N_PASS], F32, tag="bank")
            nc.tensor.matmul_mx(
                out=acc[:],
                lhsT=g_codes[:, pairs].bitcast(FP8X4),
                lhsT_scale=g_scales[:, pairs],
                rhs=w_codes[:, h_cols].bitcast(FP8X4),
                rhs_scale=w_scales[:, h_cols],
                start=True,
                stop=True,
            )
            return acc

        def multiply_quarter(t, quarter):
            pairs = slice(t * P, (t + 1) * P)
            h_cols = slice(quarter * W_GROUP_H, (quarter + 1) * W_GROUP_H)
            acc = psum.tile([P, W_GROUP_H], F32, tag="bank")
            nc.tensor.matmul_mx(
                out=acc[:],
                lhsT=g_codes[:, pairs].bitcast(FP8X4),
                lhsT_scale=g_scales[:, pairs],
                rhs=w_codes[:, h_cols].bitcast(FP8X4),
                rhs_scale=w_scales[:, h_cols],
                start=True,
                stop=True,
            )
            return acc

        def half_of(result, half):
            return result[:, half * N_PASS : (half + 1) * N_PASS]

        def turn_tile(t):
            turned = psum.tile([P, 2, P], F32, tag="bank")
            for u in range(2):
                nc.tensor.transpose(turned[:, u, :], g_row_words[:, t, u, :], identity[:])
            return turned

        def collect_tile(copy, t, turned):
            copy(
                out=g_grouped_words[:, t * P * 2 : (t + 1) * P * 2].rearrange(
                    "k (c u) -> k c u", u=2
                ),
                in_=turned[:].rearrange("k u c -> k c u"),
            )

        def quantise_tile(t):
            nc.vector.quantize_mx(
                out=g_codes[:, t * P : (t + 1) * P].bitcast(FP8X4),
                scales=g_scales[:, t * P : (t + 1) * P],
                in_=g_grouped[:, t * P * PACK : (t + 1) * P * PACK],
            )

        g_first = keep.tile([P, FIRST_TILES, F], BF16)
        g_first_words = (
            g_first[:]
            .rearrange("p t f -> p (t f)")
            .bitcast(F32)
            .rearrange("p (t k u) -> p t u k", t=FIRST_TILES, u=2)
        )

        def gate_first(t):
            adj_t = adj_cols[:, t : t + 1]
            nc.vector.tensor_scalar_mul(
                out=g_first[:, t, 0:ATOM_F], in0=atoms[:], scalar1=adj_t
            )
            nc.vector.tensor_scalar_mul(
                out=g_first[:, t, ATOM_F:ATOM_COLS], in0=atoms[:, TAIL_START:ATOM_F], scalar1=adj_t
            )

        def gate_first_bonds(t):
            nc.vector.tensor_scalar_mul(
                out=g_first[:, t, ATOM_COLS:F].rearrange("p (c w) -> p c w", c=2),
                in0=bonds[:, t * BOND_F : (t + 1) * BOND_F]
                .unsqueeze(1)
                .to_broadcast([P, 2, BOND_F]),
                scalar1=adj_cols[:, t : t + 1],
            )

        def spread_adj():
            nc.vector.tensor_copy(
                out=adj_twice[:], in_=adj_cols[:].unsqueeze(2).to_broadcast([P, TILES, 2])
            )

        def sort_atoms():
            nc.vector.tensor_copy(out=atoms_sorted[:, :, 0:ATOM_K], in_=atom_words)
            nc.vector.tensor_copy(
                out=atoms_sorted[:, :, ATOM_K:ATOMS_K], in_=atom_words[:, :, TAIL_K:ATOM_K]
            )

        def turn_first(t):
            turned = psum.tile([P, 2, P], F32, tag="bank")
            for u in range(2):
                nc.tensor.transpose(turned[:, u, :], g_first_words[:, t, u, :], identity[:])
            return turned

        warm = psum.tile([P, 4, P], F32, tag="bank")

        def keep_warm():
            nc.tensor.matmul(
                warm[:],
                lhsT=zeros[:],
                rhs=zeros[:].unsqueeze(1).to_broadcast([P, 4, P]),
                start=True,
                stop=True,
            )

        first = keep.tile([P, 2, STEP_TILES, H], F32, name="first")

        def leave(copy, t, half, acc):
            copy(out=half_of(first[:, t // 2, t % 2], half), in_=acc[:])
            nc.sync.dma_start(
                out=out_rows[:, t, half * N_PASS : (half + 1) * N_PASS],
                in_=half_of(first[:, t // 2, t % 2], half),
            )

        def leave_quarter(copy, t, quarter, acc):
            h_cols = slice(quarter * W_GROUP_H, (quarter + 1) * W_GROUP_H)
            copy(out=first[:, t // 2, t % 2, h_cols], in_=acc[:])

        def store_quarters(t, quarter):
            h_cols = slice(quarter * W_GROUP_H, (quarter + 1) * W_GROUP_H)
            nc.sync.dma_start(out=out_rows[:, t : t + 2, h_cols], in_=first[:, t // 2, :, h_cols])

        def store_quarter(t, quarter):
            h_cols = slice(quarter * W_GROUP_H, (quarter + 1) * W_GROUP_H)
            nc.sync.dma_start(out=out_rows[:, t, h_cols], in_=first[:, t // 2, t % 2, h_cols])

        for i in range(4):
            keep_warm()
        spread_adj()
        turn_first_weights(0)
        gate_first(0)
        gate_first_bonds(0)
        gate_first(1)
        gate_first_bonds(1)
        keep_warm()
        turn_first_weights(1)
        turned_0 = turn_first(0)
        turned_1 = turn_first(1)
        sort_atoms()
        gate_bonds(2, 8)
        gate_atoms(2)
        gate_atoms(3)
        collect_tile(nc.vector.tensor_copy, 0, turned_0)
        collect_tile(nc.scalar.copy, 1, turned_1)
        turned_w1 = put_weights(1)
        keep_warm()
        turned_p1 = turn(1)
        collect_weights(nc.scalar.copy, 1, turned_w1)
        quantise_weights(0)
        quantise_tile(0)
        quantise_tile(1)
        collect(nc.scalar.copy, 1, turned_p1)
        turned_w2 = put_weights(2)
        acc_q0_0 = multiply_quarter(0, 0)
        acc_q1_0 = multiply_quarter(1, 0)
        turned_w3 = put_weights(3)
        leave_quarter(nc.scalar.copy, 0, 0, acc_q0_0)
        store_quarter(0, 0)
        leave_quarter(nc.scalar.copy, 1, 0, acc_q1_0)
        store_quarter(1, 0)
        gate_atoms(4)
        gate_atoms(5)
        quantise_weights(1)
        quantise_pairs(1)
        collect_weights(nc.vector.tensor_copy, 2, turned_w2)
        collect_weights(nc.scalar.copy, 3, turned_w3)
        acc_q0_1 = multiply_quarter(0, 1)
        acc_q1_1 = multiply_quarter(1, 1)
        acc_2_0 = multiply(2, 0)
        acc_3_0 = multiply(3, 0)
        turned = turn(2)
        leave_quarter(nc.vector.tensor_copy, 0, 1, acc_q0_1)
        store_quarter(0, 1)
        leave_quarter(nc.scalar.copy, 1, 1, acc_q1_1)
        store_quarter(1, 1)
        quantise_weights(2)
        quantise_weights(3)
        leave(nc.scalar.copy, 2, 0, acc_2_0)
        leave(nc.vector.tensor_copy, 3, 0, acc_3_0)
        acc_0_1 = multiply(0, 1)
        acc_1_1 = multiply(1, 1)
        collect(nc.scalar.copy, 2, turned)
        gate_atoms(6)
        gate_atoms(7)
        acc_2_1 = multiply(2, 1)
        acc_3_1 = multiply(3, 1)
        quantise_pairs(2)
        leave(nc.scalar.copy, 0, 1, acc_0_1)
        leave(nc.vector.tensor_copy, 1, 1, acc_1_1)
        turned = turn(3)
        leave(nc.scalar.copy, 2, 1, acc_2_1)
        leave(nc.vector.tensor_copy, 3, 1, acc_3_1)
        gate_bonds(8, 16)
        gate_atoms(8)
        gate_atoms(9)

        for step in range(2, STEPS):
            result = results.tile([P, STEP_TILES, H], F32, name="result")
            if step + 1 < STEPS:
                collect(nc.scalar.copy, step + 1, turned)
            for i in range(STEP_TILES):
                t = step * STEP_TILES + i
                acc = multiply(t, 0)
                nc.vector.tensor_copy(out=half_of(result[:, i], 0), in_=acc[:])
                acc = multiply(t, 1)
                nc.scalar.copy(out=half_of(result[:, i], 1), in_=acc[:])
                if step <= 2:
                    nc.sync.dma_start(out=out_rows[:, t, :], in_=result[:, i])
                if i == 0 and step + 1 < STEPS:
                    quantise_pairs(step + 1)
            if step > 2:
                nc.sync.dma_start(
                    out=out_rows[:, step * STEP_TILES : (step + 1) * STEP_TILES, :], in_=result[:]
                )
            if step + 2 < STEPS:
                turned = turn(step + 2)
            if step + 3 < STEPS:
                gate_atoms((step + 3) * STEP_TILES)
                gate_atoms((step + 3) * STEP_TILES + 1)
